import numpy as np
import ml_dtypes


def mxq(x, axis, fmt="e4m3"):
    dtype, down = {"e4m3": (ml_dtypes.float8_e4m3fn, 7), "e5m2": (ml_dtypes.float8_e5m2, 14)}[fmt]
    v = np.moveaxis(np.asarray(x, np.float32).astype(ml_dtypes.bfloat16).astype(np.float64), axis, -1)
    blocks = v.reshape(v.shape[:-1] + (-1, 32))
    amax = np.abs(blocks).max(-1, keepdims=True)
    byte = np.maximum(np.where(amax > 0, np.frexp(amax)[1] - 1 + 127, 0) - down, 1)
    scale = np.exp2(byte - 127.0)
    codes = (blocks / scale).astype(np.float32).astype(dtype).astype(np.float64)
    return np.moveaxis((codes * scale).reshape(v.shape), -1, axis)


WIDE = False


def mx_kscale(k):
    if not WIDE:
        return np.ones(k)
    levels = np.array([10, -10, 5, -5, 0])
    a = np.random.permutation(np.resize(levels, k // 512 * 4)).reshape(k // 512, 4)
    idx = np.arange(k)
    return np.exp2(a[idx // 512, idx % 128 // 32])


BF16 = ml_dtypes.bfloat16


def bf(x):
    return np.asarray(x, np.float32).astype(BF16)


def f64(x):
    return np.asarray(x).astype(np.float64)


B, C, H, W, HID, VOCAB = 4096, 3, 84, 84, 512, 1024
EPS = 1e-8
BETA = 8


def setup_inputs():
    words = np.random.standard_normal((VOCAB, HID))
    gain = 0.5 + np.random.random((VOCAB, 1))
    near = np.random.randint(0, VOCAB, B)
    a = 0.6 + 0.35 * np.random.random((B, 1))
    q = 1.5 * (a * words[near] + np.sqrt(1.0 - a * a) * np.random.standard_normal((B, HID)))
    r = mx_kscale(HID)[np.arange(B) * HID // B][:, None]
    return {"q": bf(q * r), "word_embs": bf(words * gain), "beta": BETA}


def reference(q, word_embs, beta):
    q, e = f64(q), f64(word_embs)
    q_norm = np.sqrt((q * q).sum(-1, keepdims=True))
    e_norm = np.sqrt((e * e).sum(-1))[None, :]
    sims = (mxq(q, 1, "e4m3") @ mxq(e, 1, "e4m3").T) / (q_norm * e_norm + EPS)
    x = beta * sims
    p = np.exp(x - x.max(-1, keepdims=True))
    return (mxq(p, 1, "e4m3") @ mxq(e, 0, "e4m3")) / p.sum(-1, keepdims=True)

@@ -1,0 +1,294 @@
+import concourse.mybir as mybir
+from concourse.masks import make_identity
+
+F32 = mybir.dt.float32
+BF16 = mybir.dt.bfloat16
+U32 = mybir.dt.uint32
+U8 = mybir.dt.uint8
+FP8X4 = mybir.dt.float8_e4m3fn_x4
+ALU = mybir.AluOpType
+ACT = mybir.ActivationFunctionType
+AXIS = mybir.AxisListType
+
+P = 128
+B = 4096
+V = 1024
+HID = 512
+EPS = 1e-8
+NORM2_FLOOR = 1e-24
+
+WORDS = 256
+N_TILES = B // P
+GROUP = 4
+V_TILES = V // P
+BANK = 512
+HALVES = V // BANK
+PASSES = V // 512
+STORE = 2
+LOOKAHEAD = 6
+
+FLOPS = 2 * 2 * B * V * HID
+
+
+def contraction_to_partitions(nc, psum, copy, rows_words, grouped_words, identity):
+    chunks = rows_words.shape[1] // WORDS
+    flipped = psum.tile([P, chunks * WORDS], F32, name="flipped")
+    for piece in range(2 * chunks):
+        cols = slice(piece * P, (piece + 1) * P)
+        nc.tensor.transpose(flipped[:, cols], rows_words[:, cols], identity)
+    copy(
+        out=grouped_words.rearrange("p (c r u) -> p c r u", c=chunks, u=2),
+        in_=flipped[:].rearrange("p (c u r) -> p c r u", c=chunks, u=2),
+    )
+
+
+def tile_frozenhopfield_pa_t_kernel(tc, q, word_embs, beta, out):
+    nc = tc.nc
+    q_rows = q.rearrange("(p i) k -> p i k", i=N_TILES)
+    out_rows = out.rearrange("(p i) n -> p i n", i=N_TILES)
+
+    with (
+        tc.tile_pool(name="keep", bufs=1) as keep,
+        tc.tile_pool(name="pair", bufs=2) as pair,
+        tc.tile_pool(name="some", bufs=4) as some,
+        tc.psum_pool(name="psum_s", bufs=2) as psum_s,
+        tc.psum_pool(name="psum_t", bufs=2) as psum_t,
+        tc.psum_pool(name="psum_o", bufs=2) as psum_o,
+    ):
+        e_rows = keep.tile([P, V_TILES * HID], BF16, name="e_rows")
+        e_src = word_embs.rearrange("(t p) k -> p t k", p=P)
+        e_dst = e_rows[:].rearrange("p (t k) -> p t k", t=V_TILES)
+        for half in (slice(0, V_TILES // 2), slice(V_TILES // 2, V_TILES)):
+            nc.sync.dma_start(out=e_dst[:, half, :], in_=e_src[:, half, :])
+        q_loaded = []
+        for j in range(N_TILES // GROUP):
+            q_loaded.append(keep.tile([P, GROUP * HID], BF16, name="q_loaded%d" % j))
+
+        def load_queries(j):
+            nc.sync.dma_start(
+                out=q_loaded[j][:].rearrange("p (i k) -> p i k", i=GROUP),
+                in_=q_rows[:, j * GROUP : (j + 1) * GROUP, :],
+            )
+
+        load_queries(0)
+        load_queries(1)
+        e_by_word = keep.tile([P, V_TILES * HID], BF16, name="e_by_word")
+        nc.sync.dma_start(
+            out=e_by_word[:].rearrange("p (c e n) -> p c e n", c=4, e=2),
+            in_=word_embs.rearrange("(c p e) n -> p c e n", c=4, e=2),
+        )
+        for j in range(2, N_TILES // GROUP):
+            load_queries(j)
+
+        identity = keep.tile([P, P], F32, name="identity")
+        make_identity(nc, identity[:])
+        minus_half = keep.tile([P, V_TILES], F32, name="minus_half")
+        nc.vector.memset(minus_half[:], -0.5)
+
+        def sum_of_squares(rows, norm2):
+            squares = some.tile([P, HID], BF16, name="squares")
+            nc.scalar.activation(out=squares[:], in_=rows, func=ACT.Square, accum_out=norm2)
+
+        def inverse_norm(inv, norm2):
+            nc.gpsimd.tensor_scalar_max(out=norm2, in0=norm2, scalar1=NORM2_FLOOR)
+            nc.gpsimd.tensor_tensor(out=inv, in0=norm2, in1=minus_half[:, : norm2.shape[1]], op=ALU.pow)
+
+        e_norm2 = keep.tile([P, V_TILES], F32, name="e_norm2")
+        e_inv = keep.tile([P, V_TILES], F32, name="e_inv")
+        for t in range(V_TILES):
+            sum_of_squares(e_rows[:, t * HID : (t + 1) * HID], e_norm2[:, t : t + 1])
+        inverse_norm(e_inv[:], e_norm2[:])
+
+        e1_grouped = keep.tile([P, V * 4], BF16, name="e1_grouped", align_bytes=64)
+        e1_codes = keep.tile([P, V], U32, name="e1_codes", align_bytes=64)
+        e1_scales = keep.tile([P, V], U8, name="e1_scales", align_bytes=64)
+        for first in range(0, V_TILES * WORDS, BANK):
+            contraction_to_partitions(
+                nc, psum_t, nc.vector.tensor_copy,
+                e_rows[:].bitcast(F32)[:, first : first + BANK],
+                e1_grouped[:].bitcast(F32)[:, first : first + BANK],
+                identity[:],
+            )
+        for h in range(HALVES):
+            cols = slice(h * BANK, (h + 1) * BANK)
+            nc.vector.quantize_mx(
+                out=e1_codes[:, cols].bitcast(FP8X4),
+                scales=e1_scales[:, cols],
+                in_=e1_grouped[:, h * BANK * 4 : (h + 1) * BANK * 4],
+            )
+
+        e2_grouped = keep.tile([P, PASSES * HID * 4], BF16, name="e2_grouped", align_bytes=64)
+        e2_codes = keep.tile([P, PASSES * HID], U32, name="e2_codes", align_bytes=64)
+        e2_scales = keep.tile([P, PASSES * HID], U8, name="e2_scales", align_bytes=64)
+        for g in range(PASSES):
+            nc.vector.tensor_copy(
+                out=e2_grouped[:, g * HID * 4 : (g + 1) * HID * 4].rearrange("p (n t) -> p n t", t=4),
+                in_=e_by_word[:, g * HID * 4 : (g + 1) * HID * 4].rearrange("p (t n) -> p n t", t=4),
+            )
+        for g in range(PASSES):
+            nc.vector.quantize_mx(
+                out=e2_codes[:, g * HID : (g + 1) * HID].bitcast(FP8X4),
+                scales=e2_scales[:, g * HID : (g + 1) * HID],
+                in_=e2_grouped[:, g * HID * 4 : (g + 1) * HID * 4],
+            )
+
+        table_a = keep.tile([P, V], F32, name="table_a")
+        table_b = keep.tile([P, V], F32, name="table_b")
+        for h in range(HALVES):
+            spread = psum_s.tile([P, BANK], F32, name="spread", tag="dots%d" % h)
+            for piece in range(BANK // P):
+                t = h * (BANK // P) + piece
+                nc.tensor.matmul(
+                    out=spread[:, piece * P : (piece + 1) * P],
+                    lhsT=e_inv[:, t : t + 1].to_broadcast([P, P]),
+                    rhs=identity[:],
+                    start=True,
+                    stop=True,
+                )
+            cols = slice(h * BANK, (h + 1) * BANK)
+            nc.vector.tensor_scalar(
+                out=table_a[:, cols], in0=spread[:], scalar1=float(beta), scalar2=None, op0=ALU.mult
+            )
+            nc.vector.scalar_tensor_tensor(
+                out=table_b[:, cols], in0=table_a[:, cols], scalar=-EPS / float(beta), in1=table_a[:, cols],
+                op0=ALU.mult, op1=ALU.mult,
+            )
+
+        q_norm2, q_inv, q_grouped, q_codes, q_scales = {}, {}, {}, {}, {}
+        factor, dots, prob, row_sum, inv_sum, mixed, results = {}, {}, {}, {}, {}, {}, {}
+
+        def prepare(n):
+            j, i = divmod(n, GROUP)
+            if i == 0:
+                q_norm2[j] = keep.tile([P, GROUP], F32, name="q_norm2_%d" % j)
+                q_inv[j] = keep.tile([P, GROUP], F32, name="q_inv%d" % j)
+                q_grouped[j] = pair.tile([P, GROUP * HID], BF16, name="q_grouped", align_bytes=64)
+            sum_of_squares(q_loaded[j][:, i * HID : (i + 1) * HID], q_norm2[j][:, i : i + 1])
+            contraction_to_partitions(
+                nc, psum_t, nc.scalar.copy,
+                q_loaded[j][:].bitcast(F32)[:, i * WORDS : (i + 1) * WORDS],
+                q_grouped[j][:].bitcast(F32)[:, i * WORDS : (i + 1) * WORDS],
+                identity[:],
+            )
+
+        def quantise_group(j):
+            inverse_norm(q_inv[j][:], q_norm2[j][:])
+            q_codes[j] = keep.tile([P, GROUP * P], U32, name="q_codes%d" % j, align_bytes=64)
+            q_scales[j] = keep.tile([P, GROUP * P], U8, name="q_scales%d" % j, align_bytes=64)
+            nc.vector.quantize_mx(out=q_codes[j][:].bitcast(FP8X4), scales=q_scales[j][:], in_=q_grouped[j][:])
+
+        def inverse_query_norm(n):
+            j, i = divmod(n, GROUP)
+            return q_inv[j][:, i : i + 1]
+
+        def build_factor(n):
+            factor[n] = some.tile([P, V], F32, name="factor")
+            if n % 2 == 0:
+                nc.vector.scalar_tensor_tensor(
+                    out=factor[n][:], in0=table_b[:], scalar=inverse_query_norm(n), in1=table_a[:],
+                    op0=ALU.mult, op1=ALU.add,
+                )
+            else:
+                nc.gpsimd.tensor_scalar(
+                    out=factor[n][:], in0=table_b[:], scalar1=inverse_query_norm(n), scalar2=0.0,
+                    op0=ALU.mult, op1=ALU.add,
+                )
+                nc.gpsimd.tensor_tensor(out=factor[n][:], in0=factor[n][:], in1=table_a[:], op=ALU.add)
+
+        def scores(n):
+            j, i = divmod(n, GROUP)
+            rows = slice(i * P, (i + 1) * P)
+            dots[n] = []
+            for h in range(HALVES):
+                cols = slice(h * BANK, (h + 1) * BANK)
+                dots[n].append(psum_s.tile([P, BANK], F32, name="dots", tag="dots%d" % h))
+                nc.tensor.matmul_mx(
+                    out=dots[n][h][:],
+                    lhsT=q_codes[j][:, rows].bitcast(FP8X4),
+                    lhsT_scale=q_scales[j][:, rows],
+                    rhs=e1_codes[:, cols].bitcast(FP8X4),
+                    rhs_scale=e1_scales[:, cols],
+                    start=True,
+                    stop=True,
+                )
+
+        def logits(n):
+            x = pair.tile([P, V], F32, name="x")
+            for h in range(HALVES):
+                cols = slice(h * BANK, (h + 1) * BANK)
+                nc.vector.scalar_tensor_tensor(
+                    out=x[:, cols], in0=dots[n][h][:], scalar=inverse_query_norm(n), in1=factor[n][:, cols],
+                    op0=ALU.mult, op1=ALU.mult,
+                )
+            minus_max = pair.tile([P, 1], F32, name="minus_max")
+            nc.vector.tensor_reduce(out=minus_max[:], in_=x[:], axis=AXIS.X, op=ALU.max, negate=True)
+            prob[n] = pair.tile([P, V], BF16, name="prob")
+            row_sum[n] = some.tile([P, 1], F32, name="row_sum")
+            nc.scalar.activation(
+                out=prob[n][:], in_=x[:], func=ACT.Exp, bias=minus_max[:, 0:1], scale=1.0, accum_out=row_sum[n][:]
+            )
+
+        p_grouped = {}
+
+        def flip(n):
+            p_grouped[n] = some.tile([P, V], BF16, name="p_grouped", align_bytes=64)
+            contraction_to_partitions(
+                nc, psum_t, nc.scalar.copy, prob[n][:].bitcast(F32), p_grouped[n][:].bitcast(F32), identity[:]
+            )
+
+        def mix(n):
+            p_codes = pair.tile([P, PASSES * P], U32, name="p_codes", align_bytes=64)
+            p_scales = pair.tile([P, PASSES * P], U8, name="p_scales", align_bytes=64)
+            nc.vector.quantize_mx(out=p_codes[:].bitcast(FP8X4), scales=p_scales[:], in_=p_grouped[n][:])
+            mixed[n] = psum_o.tile([P, HID], F32, name="mixed")
+            for g in range(PASSES):
+                nc.tensor.matmul_mx(
+                    out=mixed[n][:],
+                    lhsT=p_codes[:, g * P : (g + 1) * P].bitcast(FP8X4),
+                    lhsT_scale=p_scales[:, g * P : (g + 1) * P],
+                    rhs=e2_codes[:, g * HID : (g + 1) * HID].bitcast(FP8X4),
+                    rhs_scale=e2_scales[:, g * HID : (g + 1) * HID],
+                    start=(g == 0),
+                    stop=(g == PASSES - 1),
+                )
+            inv_sum[n] = some.tile([P, 1], F32, name="inv_sum")
+            nc.vector.reciprocal(out=inv_sum[n][:], in_=row_sum[n][:])
+
+        def finish(n):
+            first, s = n - n % STORE, n % STORE
+            if s == 0:
+                results[first] = some.tile([P, STORE * HID], F32, name="results")
+            nc.scalar.activation(
+                out=results[first][:, s * HID : (s + 1) * HID], in_=mixed[n][:], func=ACT.Copy,
+                scale=inv_sum[n][:, 0:1],
+            )
+            if s == STORE - 1:
+                nc.sync.dma_start(
+                    out=out_rows[:, first : first + STORE, :],
+                    in_=results[first][:].rearrange("p (s n) -> p s n", s=STORE),
+                )
+
+        for n in range(LOOKAHEAD):
+            prepare(n)
+        quantise_group(0)
+        build_factor(0)
+        build_factor(1)
+        scores(0)
+        with tc.manual_schedule():
+            for n in range(N_TILES + 3):
+                if 0 <= n - 3:
+                    finish(n - 3)
+                if n + LOOKAHEAD < N_TILES:
+                    prepare(n + LOOKAHEAD)
+                if 0 <= n - 1 < N_TILES:
+                    flip(n - 1)
+                if n + 1 < N_TILES:
+                    scores(n + 1)
+                if n < N_TILES:
+                    logits(n)
+                if 0 <= n - 2 < N_TILES:
+                    mix(n - 2)
+                if n + LOOKAHEAD < N_TILES and (n + LOOKAHEAD) % GROUP == GROUP - 1:
+                    quantise_group((n + LOOKAHEAD) // GROUP)
+                if n + 2 < N_TILES:
+                    build_factor(n + 2)

@@ -20,12 +20,14 @@ NORM2_FLOOR = 1e-24
 WORDS = 256
 N_TILES = B // P
 GROUP = 4
+N_GROUPS = N_TILES // GROUP
 V_TILES = V // P
 BANK = 512
 HALVES = V // BANK
 PASSES = V // 512
 STORE = 2
-LOOKAHEAD = 6
+PREPARE_AHEAD = 8
+FACTOR_AHEAD = 4
 
 FLOPS = 2 * 2 * B * V * HID
 
@@ -49,8 +51,7 @@ def tile_frozenhopfield_pa_t_kernel(tc, q, word_embs, beta, out):
 
     with (
         tc.tile_pool(name="keep", bufs=1) as keep,
-        tc.tile_pool(name="pair", bufs=2) as pair,
-        tc.tile_pool(name="some", bufs=4) as some,
+        tc.tile_pool(name="ring", bufs=3) as ring,
         tc.psum_pool(name="psum_s", bufs=2) as psum_s,
         tc.psum_pool(name="psum_t", bufs=2) as psum_t,
         tc.psum_pool(name="psum_o", bufs=2) as psum_o,
@@ -61,7 +62,7 @@ def tile_frozenhopfield_pa_t_kernel(tc, q, word_embs, beta, out):
         for half in (slice(0, V_TILES // 2), slice(V_TILES // 2, V_TILES)):
             nc.sync.dma_start(out=e_dst[:, half, :], in_=e_src[:, half, :])
         q_loaded = []
-        for j in range(N_TILES // GROUP):
+        for j in range(N_GROUPS):
             q_loaded.append(keep.tile([P, GROUP * HID], BF16, name="q_loaded%d" % j))
 
         def load_queries(j):
@@ -71,13 +72,12 @@ def tile_frozenhopfield_pa_t_kernel(tc, q, word_embs, beta, out):
             )
 
         load_queries(0)
-        load_queries(1)
         e_by_word = keep.tile([P, V_TILES * HID], BF16, name="e_by_word")
         nc.sync.dma_start(
             out=e_by_word[:].rearrange("p (c e n) -> p c e n", c=4, e=2),
             in_=word_embs.rearrange("(c p e) n -> p c e n", c=4, e=2),
         )
-        for j in range(2, N_TILES // GROUP):
+        for j in range(1, N_GROUPS):
             load_queries(j)
 
         identity = keep.tile([P, P], F32, name="identity")
@@ -85,19 +85,30 @@ def tile_frozenhopfield_pa_t_kernel(tc, q, word_embs, beta, out):
         minus_half = keep.tile([P, V_TILES], F32, name="minus_half")
         nc.vector.memset(minus_half[:], -0.5)
 
-        def sum_of_squares(rows, norm2):
-            squares = some.tile([P, HID], BF16, name="squares")
+        def sum_of_squares_on_scalar(rows, norm2):
+            squares = ring.tile([P, HID], BF16, name="squares")
             nc.scalar.activation(out=squares[:], in_=rows, func=ACT.Square, accum_out=norm2)
 
-        def inverse_norm(inv, norm2):
-            nc.gpsimd.tensor_scalar_max(out=norm2, in0=norm2, scalar1=NORM2_FLOOR)
-            nc.gpsimd.tensor_tensor(out=inv, in0=norm2, in1=minus_half[:, : norm2.shape[1]], op=ALU.pow)
+        def sum_of_squares_on_vector(rows, norm2):
+            products = ring.tile([P, HID], F32, name="products")
+            nc.vector.scalar_tensor_tensor(
+                out=products[:], in0=rows, scalar=1.0, in1=rows, op0=ALU.mult, op1=ALU.mult, accum_out=norm2
+            )
 
-        e_norm2 = keep.tile([P, V_TILES], F32, name="e_norm2")
+        def inverse_norm(inv, norm2_parts):
+            first = 0
+            for part in norm2_parts:
+                nc.gpsimd.tensor_scalar_max(out=inv[:, first : first + part.shape[1]], in0=part, scalar1=NORM2_FLOOR)
+                first += part.shape[1]
+            nc.gpsimd.tensor_tensor(out=inv, in0=inv, in1=minus_half[:, :first], op=ALU.pow)
+
+        e_norm2_even = keep.tile([P, V_TILES // 2], F32, name="e_norm2_even")
+        e_norm2_odd = keep.tile([P, V_TILES // 2], F32, name="e_norm2_odd")
         e_inv = keep.tile([P, V_TILES], F32, name="e_inv")
-        for t in range(V_TILES):
-            sum_of_squares(e_rows[:, t * HID : (t + 1) * HID], e_norm2[:, t : t + 1])
-        inverse_norm(e_inv[:], e_norm2[:])
+        for t in range(0, V_TILES, 2):
+            sum_of_squares_on_scalar(e_rows[:, t * HID : (t + 1) * HID], e_norm2_even[:, t // 2 : t // 2 + 1])
+            sum_of_squares_on_vector(e_rows[:, (t + 1) * HID : (t + 2) * HID], e_norm2_odd[:, t // 2 : t // 2 + 1])
+        inverse_norm(e_inv[:], [e_norm2_even[:], e_norm2_odd[:]])
 
         e1_grouped = keep.tile([P, V * 4], BF16, name="e1_grouped", align_bytes=64)
         e1_codes = keep.tile([P, V], U32, name="e1_codes", align_bytes=64)
@@ -117,33 +128,20 @@ def tile_frozenhopfield_pa_t_kernel(tc, q, word_embs, beta, out):
                 in_=e1_grouped[:, h * BANK * 4 : (h + 1) * BANK * 4],
             )
 
-        e2_grouped = keep.tile([P, PASSES * HID * 4], BF16, name="e2_grouped", align_bytes=64)
-        e2_codes = keep.tile([P, PASSES * HID], U32, name="e2_codes", align_bytes=64)
-        e2_scales = keep.tile([P, PASSES * HID], U8, name="e2_scales", align_bytes=64)
-        for g in range(PASSES):
-            nc.vector.tensor_copy(
-                out=e2_grouped[:, g * HID * 4 : (g + 1) * HID * 4].rearrange("p (n t) -> p n t", t=4),
-                in_=e_by_word[:, g * HID * 4 : (g + 1) * HID * 4].rearrange("p (t n) -> p n t", t=4),
-            )
-        for g in range(PASSES):
-            nc.vector.quantize_mx(
-                out=e2_codes[:, g * HID : (g + 1) * HID].bitcast(FP8X4),
-                scales=e2_scales[:, g * HID : (g + 1) * HID],
-                in_=e2_grouped[:, g * HID * 4 : (g + 1) * HID * 4],
-            )
-
+        repeated = keep.tile([P, V], F32, name="repeated")
+        nc.vector.tensor_copy(
+            out=repeated[:].rearrange("p (t j) -> p t j", t=V_TILES),
+            in_=e_inv[:].unsqueeze(2).to_broadcast([P, V_TILES, P]),
+        )
         table_a = keep.tile([P, V], F32, name="table_a")
         table_b = keep.tile([P, V], F32, name="table_b")
         for h in range(HALVES):
             spread = psum_s.tile([P, BANK], F32, name="spread", tag="dots%d" % h)
             for piece in range(BANK // P):
                 t = h * (BANK // P) + piece
-                nc.tensor.matmul(
-                    out=spread[:, piece * P : (piece + 1) * P],
-                    lhsT=e_inv[:, t : t + 1].to_broadcast([P, P]),
-                    rhs=identity[:],
-                    start=True,
-                    stop=True,
+                column = t // 2 + (t % 2) * (V_TILES // 2)
+                nc.tensor.transpose(
+                    spread[:, piece * P : (piece + 1) * P], repeated[:, column * P : (column + 1) * P], identity[:]
                 )
             cols = slice(h * BANK, (h + 1) * BANK)
             nc.vector.tensor_scalar(
@@ -155,15 +153,15 @@ def tile_frozenhopfield_pa_t_kernel(tc, q, word_embs, beta, out):
             )
 
         q_norm2, q_inv, q_grouped, q_codes, q_scales = {}, {}, {}, {}, {}
-        factor, dots, prob, row_sum, inv_sum, mixed, results = {}, {}, {}, {}, {}, {}, {}
+        factor, dots, x, prob, p_grouped, row_sum, inv_sum, mixed, results = {}, {}, {}, {}, {}, {}, {}, {}, {}
 
         def prepare(n):
             j, i = divmod(n, GROUP)
             if i == 0:
                 q_norm2[j] = keep.tile([P, GROUP], F32, name="q_norm2_%d" % j)
                 q_inv[j] = keep.tile([P, GROUP], F32, name="q_inv%d" % j)
-                q_grouped[j] = pair.tile([P, GROUP * HID], BF16, name="q_grouped", align_bytes=64)
-            sum_of_squares(q_loaded[j][:, i * HID : (i + 1) * HID], q_norm2[j][:, i : i + 1])
+                q_grouped[j] = ring.tile([P, GROUP * HID], BF16, name="q_grouped", align_bytes=64)
+            sum_of_squares_on_scalar(q_loaded[j][:, i * HID : (i + 1) * HID], q_norm2[j][:, i : i + 1])
             contraction_to_partitions(
                 nc, psum_t, nc.scalar.copy,
                 q_loaded[j][:].bitcast(F32)[:, i * WORDS : (i + 1) * WORDS],
@@ -172,7 +170,7 @@ def tile_frozenhopfield_pa_t_kernel(tc, q, word_embs, beta, out):
             )
 
         def quantise_group(j):
-            inverse_norm(q_inv[j][:], q_norm2[j][:])
+            inverse_norm(q_inv[j][:], [q_norm2[j][:]])
             q_codes[j] = keep.tile([P, GROUP * P], U32, name="q_codes%d" % j, align_bytes=64)
             q_scales[j] = keep.tile([P, GROUP * P], U8, name="q_scales%d" % j, align_bytes=64)
             nc.vector.quantize_mx(out=q_codes[j][:].bitcast(FP8X4), scales=q_scales[j][:], in_=q_grouped[j][:])
@@ -182,7 +180,7 @@ def tile_frozenhopfield_pa_t_kernel(tc, q, word_embs, beta, out):
             return q_inv[j][:, i : i + 1]
 
         def build_factor(n):
-            factor[n] = some.tile([P, V], F32, name="factor")
+            factor[n] = ring.tile([P, V], F32, name="factor", bufs=FACTOR_AHEAD + 1)
             if n % 2 == 0:
                 nc.vector.scalar_tensor_tensor(
                     out=factor[n][:], in0=table_b[:], scalar=inverse_query_norm(n), in1=table_a[:],
@@ -212,33 +210,34 @@ def tile_frozenhopfield_pa_t_kernel(tc, q, word_embs, beta, out):
                     stop=True,
                 )
 
-        def logits(n):
-            x = pair.tile([P, V], F32, name="x")
+        def scale(n):
+            x[n] = ring.tile([P, V], F32, name="x")
             for h in range(HALVES):
                 cols = slice(h * BANK, (h + 1) * BANK)
                 nc.vector.scalar_tensor_tensor(
-                    out=x[:, cols], in0=dots[n][h][:], scalar=inverse_query_norm(n), in1=factor[n][:, cols],
+                    out=x[n][:, cols], in0=dots[n][h][:], scalar=inverse_query_norm(n), in1=factor[n][:, cols],
                     op0=ALU.mult, op1=ALU.mult,
                 )
-            minus_max = pair.tile([P, 1], F32, name="minus_max")
-            nc.vector.tensor_reduce(out=minus_max[:], in_=x[:], axis=AXIS.X, op=ALU.max, negate=True)
-            prob[n] = pair.tile([P, V], BF16, name="prob")
-            row_sum[n] = some.tile([P, 1], F32, name="row_sum")
+
+        def soften(n):
+            minus_max = ring.tile([P, 1], F32, name="minus_max")
+            nc.vector.tensor_reduce(out=minus_max[:], in_=x[n][:], axis=AXIS.X, op=ALU.max, negate=True)
+            prob[n] = ring.tile([P, V], BF16, name="prob")
+            row_sum[n] = ring.tile([P, 1], F32, name="row_sum", bufs=5)
             nc.scalar.activation(
-                out=prob[n][:], in_=x[:], func=ACT.Exp, bias=minus_max[:, 0:1], scale=1.0, accum_out=row_sum[n][:]
+                out=prob[n][:], in_=x[n][:], func=ACT.Exp, bias=minus_max[:, 0:1], scale=1.0,
+                accum_out=row_sum[n][:],
             )
 
-        p_grouped = {}
-
         def flip(n):
-            p_grouped[n] = some.tile([P, V], BF16, name="p_grouped", align_bytes=64)
+            p_grouped[n] = ring.tile([P, V], BF16, name="p_grouped", align_bytes=64)
             contraction_to_partitions(
                 nc, psum_t, nc.scalar.copy, prob[n][:].bitcast(F32), p_grouped[n][:].bitcast(F32), identity[:]
             )
 
         def mix(n):
-            p_codes = pair.tile([P, PASSES * P], U32, name="p_codes", align_bytes=64)
-            p_scales = pair.tile([P, PASSES * P], U8, name="p_scales", align_bytes=64)
+            p_codes = ring.tile([P, PASSES * P], U32, name="p_codes", align_bytes=64)
+            p_scales = ring.tile([P, PASSES * P], U8, name="p_scales", align_bytes=64)
             nc.vector.quantize_mx(out=p_codes[:].bitcast(FP8X4), scales=p_scales[:], in_=p_grouped[n][:])
             mixed[n] = psum_o.tile([P, HID], F32, name="mixed")
             for g in range(PASSES):
@@ -251,13 +250,13 @@ def tile_frozenhopfield_pa_t_kernel(tc, q, word_embs, beta, out):
                     start=(g == 0),
                     stop=(g == PASSES - 1),
                 )
-            inv_sum[n] = some.tile([P, 1], F32, name="inv_sum")
+            inv_sum[n] = ring.tile([P, 1], F32, name="inv_sum")
             nc.vector.reciprocal(out=inv_sum[n][:], in_=row_sum[n][:])
 
         def finish(n):
             first, s = n - n % STORE, n % STORE
             if s == 0:
-                results[first] = some.tile([P, STORE * HID], F32, name="results")
+                results[first] = ring.tile([P, STORE * HID], F32, name="results")
             nc.scalar.activation(
                 out=results[first][:, s * HID : (s + 1) * HID], in_=mixed[n][:], func=ACT.Copy,
                 scale=inv_sum[n][:, 0:1],
@@ -268,27 +267,49 @@ def tile_frozenhopfield_pa_t_kernel(tc, q, word_embs, beta, out):
                     in_=results[first][:].rearrange("p (s n) -> p s n", s=STORE),
                 )
 
-        for n in range(LOOKAHEAD):
+        for n in range(PREPARE_AHEAD):
             prepare(n)
-        quantise_group(0)
-        build_factor(0)
-        build_factor(1)
+        for j in range(PREPARE_AHEAD // GROUP):
+            quantise_group(j)
+        for n in range(FACTOR_AHEAD):
+            build_factor(n)
         scores(0)
+        scores(1)
+        scale(0)
+        scores(2)
+
+        e2_grouped = keep.tile([P, PASSES * HID * 4], BF16, name="e2_grouped", align_bytes=64)
+        e2_codes = keep.tile([P, PASSES * HID], U32, name="e2_codes", align_bytes=64)
+        e2_scales = keep.tile([P, PASSES * HID], U8, name="e2_scales", align_bytes=64)
+        for g in range(PASSES):
+            nc.scalar.copy(
+                out=e2_grouped[:, g * HID * 4 : (g + 1) * HID * 4].rearrange("p (n t) -> p n t", t=4),
+                in_=e_by_word[:, g * HID * 4 : (g + 1) * HID * 4].rearrange("p (t n) -> p n t", t=4),
+            )
+        for g in range(PASSES):
+            nc.vector.quantize_mx(
+                out=e2_codes[:, g * HID : (g + 1) * HID].bitcast(FP8X4),
+                scales=e2_scales[:, g * HID : (g + 1) * HID],
+                in_=e2_grouped[:, g * HID * 4 : (g + 1) * HID * 4],
+            )
+
         with tc.manual_schedule():
-            for n in range(N_TILES + 3):
-                if 0 <= n - 3:
-                    finish(n - 3)
-                if n + LOOKAHEAD < N_TILES:
-                    prepare(n + LOOKAHEAD)
-                if 0 <= n - 1 < N_TILES:
-                    flip(n - 1)
-                if n + 1 < N_TILES:
-                    scores(n + 1)
-                if n < N_TILES:
-                    logits(n)
+            for n in range(N_TILES + 4):
+                if 0 <= n - 4:
+                    finish(n - 4)
                 if 0 <= n - 2 < N_TILES:
-                    mix(n - 2)
-                if n + LOOKAHEAD < N_TILES and (n + LOOKAHEAD) % GROUP == GROUP - 1:
-                    quantise_group((n + LOOKAHEAD) // GROUP)
-                if n + 2 < N_TILES:
-                    build_factor(n + 2)
+                    flip(n - 2)
+                if n + PREPARE_AHEAD < N_TILES:
+                    prepare(n + PREPARE_AHEAD)
+                if n + 1 < N_TILES:
+                    scale(n + 1)
+                if n + 3 < N_TILES:
+                    scores(n + 3)
+                if n < N_TILES:
+                    soften(n)
+                if 0 <= n - 3 < N_TILES:
+                    mix(n - 3)
+                if n + FACTOR_AHEAD < N_TILES:
+                    build_factor(n + FACTOR_AHEAD)
+                if n + PREPARE_AHEAD < N_TILES and (n + PREPARE_AHEAD) % GROUP == GROUP - 1:
+                    quantise_group((n + PREPARE_AHEAD) // GROUP)

@@ -28,6 +28,7 @@ PASSES = V // 512
 STORE = 2
 PREPARE_AHEAD = 8
 FACTOR_AHEAD = 4
+VECTOR_SHARE = 3
 
 FLOPS = 2 * 2 * B * V * HID
 
@@ -181,7 +182,7 @@ def tile_frozenhopfield_pa_t_kernel(tc, q, word_embs, beta, out):
 
         def build_factor(n):
             factor[n] = ring.tile([P, V], F32, name="factor", bufs=FACTOR_AHEAD + 1)
-            if n % 2 == 0:
+            if n % VECTOR_SHARE == 0:
                 nc.vector.scalar_tensor_tensor(
                     out=factor[n][:], in0=table_b[:], scalar=inverse_query_norm(n), in1=table_a[:],
                     op0=ALU.mult, op1=ALU.add,

@@ -28,7 +28,7 @@ PASSES = V // 512
 STORE = 2
 PREPARE_AHEAD = 8
 FACTOR_AHEAD = 4
-VECTOR_SHARE = 3
+GPSIMD_SHARE = 3
 
 FLOPS = 2 * 2 * B * V * HID
 
@@ -182,7 +182,7 @@ def tile_frozenhopfield_pa_t_kernel(tc, q, word_embs, beta, out):
 
         def build_factor(n):
             factor[n] = ring.tile([P, V], F32, name="factor", bufs=FACTOR_AHEAD + 1)
-            if n % VECTOR_SHARE == 0:
+            if n % GPSIMD_SHARE != 1:
                 nc.vector.scalar_tensor_tensor(
                     out=factor[n][:], in0=table_b[:], scalar=inverse_query_norm(n), in1=table_a[:],
                     op0=ALU.mult, op1=ALU.add,

@@ -19,30 +19,37 @@ NORM2_FLOOR = 1e-24
 
 WORDS = 256
 N_TILES = B // P
-GROUP = 4
-N_GROUPS = N_TILES // GROUP
+PAIR = 2
+N_PAIRS = N_TILES // PAIR
+PQ = PAIR * P
 V_TILES = V // P
 BANK = 512
 HALVES = V // BANK
 PASSES = V // 512
-STORE = 2
-PREPARE_AHEAD = 8
-FACTOR_AHEAD = 4
-GPSIMD_SHARE = 3
+VECTOR_COLS = 256
+PIECE = 256
 
 FLOPS = 2 * 2 * B * V * HID
 
 
 def contraction_to_partitions(nc, psum, copy, rows_words, grouped_words, identity):
+    flip_rows(nc, psum, rows_words, identity)(copy, grouped_words)
+
+
+def flip_rows(nc, psum, rows_words, identity):
     chunks = rows_words.shape[1] // WORDS
     flipped = psum.tile([P, chunks * WORDS], F32, name="flipped")
     for piece in range(2 * chunks):
         cols = slice(piece * P, (piece + 1) * P)
         nc.tensor.transpose(flipped[:, cols], rows_words[:, cols], identity)
-    copy(
-        out=grouped_words.rearrange("p (c r u) -> p c r u", c=chunks, u=2),
-        in_=flipped[:].rearrange("p (c u r) -> p c r u", c=chunks, u=2),
-    )
+
+    def copy_out(copy, grouped_words):
+        copy(
+            out=grouped_words.rearrange("p (c r u) -> p c r u", c=chunks, u=2),
+            in_=flipped[:].rearrange("p (c u r) -> p c r u", c=chunks, u=2),
+        )
+
+    return copy_out
 
 
 def tile_frozenhopfield_pa_t_kernel(tc, q, word_embs, beta, out):
@@ -53,32 +60,36 @@ def tile_frozenhopfield_pa_t_kernel(tc, q, word_embs, beta, out):
     with (
         tc.tile_pool(name="keep", bufs=1) as keep,
         tc.tile_pool(name="ring", bufs=3) as ring,
-        tc.psum_pool(name="psum_s", bufs=2) as psum_s,
+        tc.psum_pool(name="psum_b", bufs=1) as psum_b,
+        tc.psum_pool(name="psum_s", bufs=3) as psum_s,
         tc.psum_pool(name="psum_t", bufs=2) as psum_t,
         tc.psum_pool(name="psum_o", bufs=2) as psum_o,
+        tc.manual_schedule(),
     ):
-        e_rows = keep.tile([P, V_TILES * HID], BF16, name="e_rows")
-        e_src = word_embs.rearrange("(t p) k -> p t k", p=P)
-        e_dst = e_rows[:].rearrange("p (t k) -> p t k", t=V_TILES)
-        for half in (slice(0, V_TILES // 2), slice(V_TILES // 2, V_TILES)):
-            nc.sync.dma_start(out=e_dst[:, half, :], in_=e_src[:, half, :])
         q_loaded = []
-        for j in range(N_GROUPS):
-            q_loaded.append(keep.tile([P, GROUP * HID], BF16, name="q_loaded%d" % j))
+        for j in range(N_PAIRS):
+            q_loaded.append(keep.tile([P, PAIR * HID], BF16, name="q_loaded%d" % j))
 
         def load_queries(j):
             nc.sync.dma_start(
-                out=q_loaded[j][:].rearrange("p (i k) -> p i k", i=GROUP),
-                in_=q_rows[:, j * GROUP : (j + 1) * GROUP, :],
+                out=q_loaded[j][:].rearrange("p (i k) -> p i k", i=PAIR),
+                in_=q_rows[:, j * PAIR : (j + 1) * PAIR, :],
             )
 
+        e_rows = keep.tile([P, V_TILES * HID], BF16, name="e_rows")
+        e_src = word_embs.rearrange("(t p) k -> p t k", p=P)
+        e_dst = e_rows[:].rearrange("p (t k) -> p t k", t=V_TILES)
+        for quarter in range(4):
+            tiles = slice(2 * quarter, 2 * quarter + 2)
+            nc.sync.dma_start(out=e_dst[:, tiles, :], in_=e_src[:, tiles, :])
         load_queries(0)
+        load_queries(1)
         e_by_word = keep.tile([P, V_TILES * HID], BF16, name="e_by_word")
         nc.sync.dma_start(
             out=e_by_word[:].rearrange("p (c e n) -> p c e n", c=4, e=2),
             in_=word_embs.rearrange("(c p e) n -> p c e n", c=4, e=2),
         )
-        for j in range(1, N_GROUPS):
+        for j in range(2, N_PAIRS):
             load_queries(j)
 
         identity = keep.tile([P, P], F32, name="identity")
@@ -96,31 +107,34 @@ def tile_frozenhopfield_pa_t_kernel(tc, q, word_embs, beta, out):
                 out=products[:], in0=rows, scalar=1.0, in1=rows, op0=ALU.mult, op1=ALU.mult, accum_out=norm2
             )
 
-        def inverse_norm(inv, norm2_parts):
-            first = 0
-            for part in norm2_parts:
-                nc.gpsimd.tensor_scalar_max(out=inv[:, first : first + part.shape[1]], in0=part, scalar1=NORM2_FLOOR)
-                first += part.shape[1]
-            nc.gpsimd.tensor_tensor(out=inv, in0=inv, in1=minus_half[:, :first], op=ALU.pow)
-
         e_norm2_even = keep.tile([P, V_TILES // 2], F32, name="e_norm2_even")
         e_norm2_odd = keep.tile([P, V_TILES // 2], F32, name="e_norm2_odd")
         e_inv = keep.tile([P, V_TILES], F32, name="e_inv")
-        for t in range(0, V_TILES, 2):
-            sum_of_squares_on_scalar(e_rows[:, t * HID : (t + 1) * HID], e_norm2_even[:, t // 2 : t // 2 + 1])
-            sum_of_squares_on_vector(e_rows[:, (t + 1) * HID : (t + 2) * HID], e_norm2_odd[:, t // 2 : t // 2 + 1])
-        inverse_norm(e_inv[:], [e_norm2_even[:], e_norm2_odd[:]])
+        e_inv2 = keep.tile([P, V_TILES], F32, name="e_inv2")
+
+        def column(t):
+            c = t // 2 + (t % 2) * (V_TILES // 2)
+            return slice(c, c + 1)
 
         e1_grouped = keep.tile([P, V * 4], BF16, name="e1_grouped", align_bytes=64)
         e1_codes = keep.tile([P, V], U32, name="e1_codes", align_bytes=64)
         e1_scales = keep.tile([P, V], U8, name="e1_scales", align_bytes=64)
-        for first in range(0, V_TILES * WORDS, BANK):
+        for c in range(V_TILES // 2):
+            sum_of_squares_on_scalar(e_rows[:, 2 * c * HID : (2 * c + 1) * HID], e_norm2_even[:, c : c + 1])
+            sum_of_squares_on_vector(e_rows[:, (2 * c + 1) * HID : (2 * c + 2) * HID], e_norm2_odd[:, c : c + 1])
+        for c in range(V_TILES // 2):
+            first = c * BANK
             contraction_to_partitions(
-                nc, psum_t, nc.vector.tensor_copy,
+                nc, psum_t, nc.scalar.copy if c % 2 else nc.vector.tensor_copy,
                 e_rows[:].bitcast(F32)[:, first : first + BANK],
                 e1_grouped[:].bitcast(F32)[:, first : first + BANK],
                 identity[:],
             )
+        half = V_TILES // 2
+        nc.gpsimd.tensor_scalar_max(out=e_inv[:, :half], in0=e_norm2_even[:], scalar1=NORM2_FLOOR)
+        nc.gpsimd.tensor_scalar_max(out=e_inv[:, half:], in0=e_norm2_odd[:], scalar1=NORM2_FLOOR)
+        nc.gpsimd.tensor_tensor(out=e_inv[:], in0=e_inv[:], in1=minus_half[:], op=ALU.pow)
+        nc.gpsimd.tensor_tensor(out=e_inv2[:], in0=e_inv[:], in1=e_inv[:], op=ALU.mult)
         for h in range(HALVES):
             cols = slice(h * BANK, (h + 1) * BANK)
             nc.vector.quantize_mx(
@@ -129,188 +143,245 @@ def tile_frozenhopfield_pa_t_kernel(tc, q, word_embs, beta, out):
                 in_=e1_grouped[:, h * BANK * 4 : (h + 1) * BANK * 4],
             )
 
-        repeated = keep.tile([P, V], F32, name="repeated")
-        nc.vector.tensor_copy(
-            out=repeated[:].rearrange("p (t j) -> p t j", t=V_TILES),
-            in_=e_inv[:].unsqueeze(2).to_broadcast([P, V_TILES, P]),
-        )
+        q_norm2, q_inv, q_grouped, q_codes, q_scales = {}, {}, {}, {}, {}
+
+        def square_queries(n):
+            j, i = divmod(n, PAIR)
+            if i == 0:
+                q_norm2[j] = keep.tile([P, PAIR], F32, name="q_norm2_%d" % j)
+            sum_of_squares_on_scalar(q_loaded[j][:, i * HID : (i + 1) * HID], q_norm2[j][:, i : i + 1])
+
+        def flip_queries(j):
+            q_grouped[j] = ring.tile([P, PAIR * HID], BF16, name="q_grouped", align_bytes=64)
+            contraction_to_partitions(
+                nc, psum_t, nc.scalar.copy, q_loaded[j][:].bitcast(F32), q_grouped[j][:].bitcast(F32), identity[:]
+            )
+
+        def query_norms(j):
+            q_inv[j] = keep.tile([P, PAIR], F32, name="q_inv%d" % j)
+            nc.gpsimd.tensor_scalar_max(out=q_inv[j][:], in0=q_norm2[j][:], scalar1=NORM2_FLOOR)
+            nc.gpsimd.tensor_tensor(out=q_inv[j][:], in0=q_inv[j][:], in1=minus_half[:, :PAIR], op=ALU.pow)
+
+        def quantise_queries(j):
+            q_codes[j] = ring.tile([P, PQ], U32, name="q_codes", align_bytes=64)
+            q_scales[j] = ring.tile([P, PQ], U8, name="q_scales", align_bytes=64)
+            nc.vector.quantize_mx(out=q_codes[j][:].bitcast(FP8X4), scales=q_scales[j][:], in_=q_grouped[j][:])
+
+        square_queries(0)
+        square_queries(1)
+        flip_queries(0)
+        query_norms(0)
+
         table_a = keep.tile([P, V], F32, name="table_a")
         table_b = keep.tile([P, V], F32, name="table_b")
+        inv2_psum = psum_b.tile([P, BANK], F32, name="inv2_psum")
         for h in range(HALVES):
-            spread = psum_s.tile([P, BANK], F32, name="spread", tag="dots%d" % h)
-            for piece in range(BANK // P):
-                t = h * (BANK // P) + piece
-                column = t // 2 + (t % 2) * (V_TILES // 2)
+            spread = psum_s.tile([P, BANK], F32, name="spread", tag="dots")
+            for s in range(BANK // P):
                 nc.tensor.transpose(
-                    spread[:, piece * P : (piece + 1) * P], repeated[:, column * P : (column + 1) * P], identity[:]
+                    spread[:, s * P : (s + 1) * P],
+                    e_inv[:, column(h * (BANK // P) + s)].to_broadcast([P, P]), identity[:],
                 )
             cols = slice(h * BANK, (h + 1) * BANK)
             nc.vector.tensor_scalar(
                 out=table_a[:, cols], in0=spread[:], scalar1=float(beta), scalar2=None, op0=ALU.mult
             )
+        for h in range(HALVES):
+            spread = inv2_psum if h == 0 else psum_s.tile([P, BANK], F32, name="spread", tag="dots")
+            for s in range(BANK // P):
+                nc.tensor.transpose(
+                    spread[:, s * P : (s + 1) * P],
+                    e_inv2[:, column(h * (BANK // P) + s)].to_broadcast([P, P]), identity[:],
+                )
+            cols = slice(h * BANK, (h + 1) * BANK)
+            nc.scalar.activation(out=table_b[:, cols], in_=spread[:], func=ACT.Copy, scale=-EPS * float(beta))
+
+        factor, dots, x, minus_max, prob, p_flip, p_grouped, p_codes, p_scales = {}, {}, {}, {}, {}, {}, {}, {}, {}
+        row_sum, inv_sum, mixed, results, q_minus = {}, {}, {}, {}, {}
+
+        def inverse_query_norm(n):
+            j, i = divmod(n, PAIR)
+            return q_inv[j][:, i : i + 1]
+
+        def factor_on_gpsimd(n):
+            factor[n] = ring.tile([P, V], F32, name="factor", bufs=4)
+            if n == 0:
+                return
+            pieces = []
+            for first in range(VECTOR_COLS, V, PIECE):
+                pieces.append(slice(first, min(first + PIECE, V)))
+            for cols in pieces:
+                nc.gpsimd.tensor_scalar(
+                    out=factor[n][:, cols], in0=table_b[:, cols], scalar1=inverse_query_norm(n), scalar2=0.0,
+                    op0=ALU.mult, op1=ALU.add,
+                )
+            for cols in pieces:
+                nc.gpsimd.tensor_tensor(
+                    out=factor[n][:, cols], in0=factor[n][:, cols], in1=table_a[:, cols], op=ALU.add
+                )
+
+        def factor_on_vector(n):
+            cols = slice(0, VECTOR_COLS)
             nc.vector.scalar_tensor_tensor(
-                out=table_b[:, cols], in0=table_a[:, cols], scalar=-EPS / float(beta), in1=table_a[:, cols],
+                out=factor[n][:, cols], in0=inv2_psum[:, cols], scalar=q_minus[n // PAIR][:, n % PAIR : n % PAIR + 1],
+                in1=table_a[:, cols], op0=ALU.mult, op1=ALU.add,
+            )
+            if n == 0:
+                cols = slice(VECTOR_COLS, V)
+                nc.vector.scalar_tensor_tensor(
+                    out=factor[n][:, cols], in0=table_b[:, cols], scalar=inverse_query_norm(n), in1=table_a[:, cols],
+                    op0=ALU.mult, op1=ALU.add,
+                )
+
+        def minus_query_norms(j):
+            q_minus[j] = keep.tile([P, PAIR], F32, name="q_minus%d" % j)
+            nc.gpsimd.tensor_scalar(
+                out=q_minus[j][:], in0=q_inv[j][:], scalar1=-EPS * float(beta), scalar2=0.0,
+                op0=ALU.mult, op1=ALU.add,
+            )
+
+        def scores(n, h):
+            j, i = divmod(n, PAIR)
+            rows = slice(i * P, (i + 1) * P)
+            cols = slice(h * BANK, (h + 1) * BANK)
+            dots[n, h] = psum_s.tile([P, BANK], F32, name="dots")
+            nc.tensor.matmul_mx(
+                out=dots[n, h][:],
+                lhsT=q_codes[j][:, rows].bitcast(FP8X4),
+                lhsT_scale=q_scales[j][:, rows],
+                rhs=e1_codes[:, cols].bitcast(FP8X4),
+                rhs_scale=e1_scales[:, cols],
+                start=True,
+                stop=True,
+            )
+
+        def scale(n, h):
+            if h == 0:
+                x[n] = ring.tile([P, V], F32, name="x")
+            cols = slice(h * BANK, (h + 1) * BANK)
+            nc.vector.scalar_tensor_tensor(
+                out=x[n][:, cols], in0=dots[n, h][:], scalar=inverse_query_norm(n), in1=factor[n][:, cols],
                 op0=ALU.mult, op1=ALU.mult,
             )
 
-        q_norm2, q_inv, q_grouped, q_codes, q_scales = {}, {}, {}, {}, {}
-        factor, dots, x, prob, p_grouped, row_sum, inv_sum, mixed, results = {}, {}, {}, {}, {}, {}, {}, {}, {}
-
-        def prepare(n):
-            j, i = divmod(n, GROUP)
-            if i == 0:
-                q_norm2[j] = keep.tile([P, GROUP], F32, name="q_norm2_%d" % j)
-                q_inv[j] = keep.tile([P, GROUP], F32, name="q_inv%d" % j)
-                q_grouped[j] = ring.tile([P, GROUP * HID], BF16, name="q_grouped", align_bytes=64)
-            sum_of_squares_on_scalar(q_loaded[j][:, i * HID : (i + 1) * HID], q_norm2[j][:, i : i + 1])
-            contraction_to_partitions(
-                nc, psum_t, nc.scalar.copy,
-                q_loaded[j][:].bitcast(F32)[:, i * WORDS : (i + 1) * WORDS],
-                q_grouped[j][:].bitcast(F32)[:, i * WORDS : (i + 1) * WORDS],
-                identity[:],
-            )
-
-        def quantise_group(j):
-            inverse_norm(q_inv[j][:], [q_norm2[j][:]])
-            q_codes[j] = keep.tile([P, GROUP * P], U32, name="q_codes%d" % j, align_bytes=64)
-            q_scales[j] = keep.tile([P, GROUP * P], U8, name="q_scales%d" % j, align_bytes=64)
-            nc.vector.quantize_mx(out=q_codes[j][:].bitcast(FP8X4), scales=q_scales[j][:], in_=q_grouped[j][:])
-
-        def inverse_query_norm(n):
-            j, i = divmod(n, GROUP)
-            return q_inv[j][:, i : i + 1]
-
-        def build_factor(n):
-            factor[n] = ring.tile([P, V], F32, name="factor", bufs=FACTOR_AHEAD + 1)
-            if n % GPSIMD_SHARE != 1:
-                nc.vector.scalar_tensor_tensor(
-                    out=factor[n][:], in0=table_b[:], scalar=inverse_query_norm(n), in1=table_a[:],
-                    op0=ALU.mult, op1=ALU.add,
-                )
-            else:
-                nc.gpsimd.tensor_scalar(
-                    out=factor[n][:], in0=table_b[:], scalar1=inverse_query_norm(n), scalar2=0.0,
-                    op0=ALU.mult, op1=ALU.add,
-                )
-                nc.gpsimd.tensor_tensor(out=factor[n][:], in0=factor[n][:], in1=table_a[:], op=ALU.add)
-
-        def scores(n):
-            j, i = divmod(n, GROUP)
-            rows = slice(i * P, (i + 1) * P)
-            dots[n] = []
-            for h in range(HALVES):
-                cols = slice(h * BANK, (h + 1) * BANK)
-                dots[n].append(psum_s.tile([P, BANK], F32, name="dots", tag="dots%d" % h))
-                nc.tensor.matmul_mx(
-                    out=dots[n][h][:],
-                    lhsT=q_codes[j][:, rows].bitcast(FP8X4),
-                    lhsT_scale=q_scales[j][:, rows],
-                    rhs=e1_codes[:, cols].bitcast(FP8X4),
-                    rhs_scale=e1_scales[:, cols],
-                    start=True,
-                    stop=True,
-                )
-
-        def scale(n):
-            x[n] = ring.tile([P, V], F32, name="x")
-            for h in range(HALVES):
-                cols = slice(h * BANK, (h + 1) * BANK)
-                nc.vector.scalar_tensor_tensor(
-                    out=x[n][:, cols], in0=dots[n][h][:], scalar=inverse_query_norm(n), in1=factor[n][:, cols],
-                    op0=ALU.mult, op1=ALU.mult,
-                )
+        def row_maximum(n):
+            minus_max[n] = ring.tile([P, 1], F32, name="minus_max")
+            nc.vector.tensor_reduce(out=minus_max[n][:], in_=x[n][:], axis=AXIS.X, op=ALU.max, negate=True)
 
         def soften(n):
-            minus_max = ring.tile([P, 1], F32, name="minus_max")
-            nc.vector.tensor_reduce(out=minus_max[:], in_=x[n][:], axis=AXIS.X, op=ALU.max, negate=True)
+            j, i = divmod(n, PAIR)
+            if i == 0:
+                row_sum[j] = ring.tile([P, PAIR], F32, name="row_sum")
             prob[n] = ring.tile([P, V], BF16, name="prob")
-            row_sum[n] = ring.tile([P, 1], F32, name="row_sum", bufs=5)
             nc.scalar.activation(
-                out=prob[n][:], in_=x[n][:], func=ACT.Exp, bias=minus_max[:, 0:1], scale=1.0,
-                accum_out=row_sum[n][:],
+                out=prob[n][:], in_=x[n][:], func=ACT.Exp, bias=minus_max[n][:], scale=1.0,
+                accum_out=row_sum[j][:, i : i + 1],
             )
 
-        def flip(n):
+        def flip_prob(n):
+            p_flip[n] = flip_rows(nc, psum_t, prob[n][:].bitcast(F32), identity[:])
+
+        def group_prob(n):
             p_grouped[n] = ring.tile([P, V], BF16, name="p_grouped", align_bytes=64)
-            contraction_to_partitions(
-                nc, psum_t, nc.scalar.copy, prob[n][:].bitcast(F32), p_grouped[n][:].bitcast(F32), identity[:]
-            )
+            p_flip[n](nc.scalar.copy, p_grouped[n][:].bitcast(F32))
+
+        def quantise_prob(n):
+            p_codes[n] = ring.tile([P, PASSES * P], U32, name="p_codes", align_bytes=64)
+            p_scales[n] = ring.tile([P, PASSES * P], U8, name="p_scales", align_bytes=64)
+            nc.vector.quantize_mx(out=p_codes[n][:].bitcast(FP8X4), scales=p_scales[n][:], in_=p_grouped[n][:])
+
+        def invert_sums(j):
+            inv_sum[j] = ring.tile([P, PAIR], F32, name="inv_sum")
+            nc.vector.reciprocal(out=inv_sum[j][:], in_=row_sum[j][:])
 
         def mix(n):
-            p_codes = ring.tile([P, PASSES * P], U32, name="p_codes", align_bytes=64)
-            p_scales = ring.tile([P, PASSES * P], U8, name="p_scales", align_bytes=64)
-            nc.vector.quantize_mx(out=p_codes[:].bitcast(FP8X4), scales=p_scales[:], in_=p_grouped[n][:])
             mixed[n] = psum_o.tile([P, HID], F32, name="mixed")
             for g in range(PASSES):
                 nc.tensor.matmul_mx(
                     out=mixed[n][:],
-                    lhsT=p_codes[:, g * P : (g + 1) * P].bitcast(FP8X4),
-                    lhsT_scale=p_scales[:, g * P : (g + 1) * P],
+                    lhsT=p_codes[n][:, g * P : (g + 1) * P].bitcast(FP8X4),
+                    lhsT_scale=p_scales[n][:, g * P : (g + 1) * P],
                     rhs=e2_codes[:, g * HID : (g + 1) * HID].bitcast(FP8X4),
                     rhs_scale=e2_scales[:, g * HID : (g + 1) * HID],
                     start=(g == 0),
                     stop=(g == PASSES - 1),
                 )
-            inv_sum[n] = ring.tile([P, 1], F32, name="inv_sum")
-            nc.vector.reciprocal(out=inv_sum[n][:], in_=row_sum[n][:])
 
         def finish(n):
-            first, s = n - n % STORE, n % STORE
-            if s == 0:
-                results[first] = ring.tile([P, STORE * HID], F32, name="results")
+            j, i = divmod(n, PAIR)
+            if i == 0:
+                results[j] = ring.tile([P, PAIR * HID], F32, name="results")
             nc.scalar.activation(
-                out=results[first][:, s * HID : (s + 1) * HID], in_=mixed[n][:], func=ACT.Copy,
-                scale=inv_sum[n][:, 0:1],
+                out=results[j][:, i * HID : (i + 1) * HID], in_=mixed[n][:], func=ACT.Copy,
+                scale=inv_sum[j][:, i : i + 1],
             )
-            if s == STORE - 1:
+            if i == PAIR - 1:
                 nc.sync.dma_start(
-                    out=out_rows[:, first : first + STORE, :],
-                    in_=results[first][:].rearrange("p (s n) -> p s n", s=STORE),
+                    out=out_rows[:, j * PAIR : (j + 1) * PAIR, :],
+                    in_=results[j][:].rearrange("p (s n) -> p s n", s=PAIR),
                 )
-
-        for n in range(PREPARE_AHEAD):
-            prepare(n)
-        for j in range(PREPARE_AHEAD // GROUP):
-            quantise_group(j)
-        for n in range(FACTOR_AHEAD):
-            build_factor(n)
-        scores(0)
-        scores(1)
-        scale(0)
-        scores(2)
 
         e2_grouped = keep.tile([P, PASSES * HID * 4], BF16, name="e2_grouped", align_bytes=64)
         e2_codes = keep.tile([P, PASSES * HID], U32, name="e2_codes", align_bytes=64)
         e2_scales = keep.tile([P, PASSES * HID], U8, name="e2_scales", align_bytes=64)
-        for g in range(PASSES):
+
+        def group_words(g):
             nc.scalar.copy(
                 out=e2_grouped[:, g * HID * 4 : (g + 1) * HID * 4].rearrange("p (n t) -> p n t", t=4),
                 in_=e_by_word[:, g * HID * 4 : (g + 1) * HID * 4].rearrange("p (t n) -> p n t", t=4),
             )
-        for g in range(PASSES):
+
+        def quantise_words(g):
             nc.vector.quantize_mx(
                 out=e2_codes[:, g * HID : (g + 1) * HID].bitcast(FP8X4),
                 scales=e2_scales[:, g * HID : (g + 1) * HID],
                 in_=e2_grouped[:, g * HID * 4 : (g + 1) * HID * 4],
             )
 
-        with tc.manual_schedule():
-            for n in range(N_TILES + 4):
-                if 0 <= n - 4:
-                    finish(n - 4)
-                if 0 <= n - 2 < N_TILES:
-                    flip(n - 2)
-                if n + PREPARE_AHEAD < N_TILES:
-                    prepare(n + PREPARE_AHEAD)
-                if n + 1 < N_TILES:
-                    scale(n + 1)
-                if n + 3 < N_TILES:
-                    scores(n + 3)
-                if n < N_TILES:
-                    soften(n)
-                if 0 <= n - 3 < N_TILES:
-                    mix(n - 3)
-                if n + FACTOR_AHEAD < N_TILES:
-                    build_factor(n + FACTOR_AHEAD)
-                if n + PREPARE_AHEAD < N_TILES and (n + PREPARE_AHEAD) % GROUP == GROUP - 1:
-                    quantise_group((n + PREPARE_AHEAD) // GROUP)
+        def tile_exists(n):
+            return 0 <= n < N_TILES
+
+        def pair_exists(j):
+            return 0 <= j < N_PAIRS
+
+        for n in range(-4, N_TILES + 5):
+            k, i = divmod(n, PAIR)
+            if tile_exists(n - 1):
+                soften(n - 1)
+            if tile_exists(n - 4):
+                mix(n - 4)
+                finish(n - 4)
+            if pair_exists(k + 2) and i == 0:
+                if k + 2 > 0:
+                    query_norms(k + 2)
+                minus_query_norms(k + 2)
+            if tile_exists(n + 3):
+                factor_on_gpsimd(n + 3)
+            if tile_exists(n + 1):
+                scale(n + 1, 0)
+                scale(n + 1, 1)
+            if tile_exists(n + 2):
+                scores(n + 2, 0)
+                scores(n + 2, 1)
+            if tile_exists(n):
+                row_maximum(n)
+            if tile_exists(n - 2):
+                flip_prob(n - 2)
+            if tile_exists(n + 6):
+                square_queries(n + 6)
+            if tile_exists(n - 2):
+                group_prob(n - 2)
+            if pair_exists(k + 3) and i == 1:
+                flip_queries(k + 3)
+            if tile_exists(n - 3):
+                quantise_prob(n - 3)
+            if tile_exists(n + 2):
+                factor_on_vector(n + 2)
+            if pair_exists(k + 2) and i == 0:
+                quantise_queries(k + 2)
+            if i == 1 and pair_exists(k - 1):
+                invert_sums(k - 1)
+            if n in (-2, 1):
+                group_words(0 if n == -2 else 1)
+            if n in (2, 3):
+                quantise_words(n - 2)

@@ -26,8 +26,8 @@ V_TILES = V // P
 BANK = 512
 HALVES = V // BANK
 PASSES = V // 512
-VECTOR_COLS = 256
-PIECE = 256
+VECTOR_COLS = 512
+PIECE = 512
 
 FLOPS = 2 * 2 * B * V * HID
 
@@ -60,8 +60,7 @@ def tile_frozenhopfield_pa_t_kernel(tc, q, word_embs, beta, out):
     with (
         tc.tile_pool(name="keep", bufs=1) as keep,
         tc.tile_pool(name="ring", bufs=3) as ring,
-        tc.psum_pool(name="psum_b", bufs=1) as psum_b,
-        tc.psum_pool(name="psum_s", bufs=3) as psum_s,
+        tc.psum_pool(name="psum_s", bufs=4) as psum_s,
         tc.psum_pool(name="psum_t", bufs=2) as psum_t,
         tc.psum_pool(name="psum_o", bufs=2) as psum_o,
         tc.manual_schedule(),
@@ -107,42 +106,6 @@ def tile_frozenhopfield_pa_t_kernel(tc, q, word_embs, beta, out):
                 out=products[:], in0=rows, scalar=1.0, in1=rows, op0=ALU.mult, op1=ALU.mult, accum_out=norm2
             )
 
-        e_norm2_even = keep.tile([P, V_TILES // 2], F32, name="e_norm2_even")
-        e_norm2_odd = keep.tile([P, V_TILES // 2], F32, name="e_norm2_odd")
-        e_inv = keep.tile([P, V_TILES], F32, name="e_inv")
-        e_inv2 = keep.tile([P, V_TILES], F32, name="e_inv2")
-
-        def column(t):
-            c = t // 2 + (t % 2) * (V_TILES // 2)
-            return slice(c, c + 1)
-
-        e1_grouped = keep.tile([P, V * 4], BF16, name="e1_grouped", align_bytes=64)
-        e1_codes = keep.tile([P, V], U32, name="e1_codes", align_bytes=64)
-        e1_scales = keep.tile([P, V], U8, name="e1_scales", align_bytes=64)
-        for c in range(V_TILES // 2):
-            sum_of_squares_on_scalar(e_rows[:, 2 * c * HID : (2 * c + 1) * HID], e_norm2_even[:, c : c + 1])
-            sum_of_squares_on_vector(e_rows[:, (2 * c + 1) * HID : (2 * c + 2) * HID], e_norm2_odd[:, c : c + 1])
-        for c in range(V_TILES // 2):
-            first = c * BANK
-            contraction_to_partitions(
-                nc, psum_t, nc.scalar.copy if c % 2 else nc.vector.tensor_copy,
-                e_rows[:].bitcast(F32)[:, first : first + BANK],
-                e1_grouped[:].bitcast(F32)[:, first : first + BANK],
-                identity[:],
-            )
-        half = V_TILES // 2
-        nc.gpsimd.tensor_scalar_max(out=e_inv[:, :half], in0=e_norm2_even[:], scalar1=NORM2_FLOOR)
-        nc.gpsimd.tensor_scalar_max(out=e_inv[:, half:], in0=e_norm2_odd[:], scalar1=NORM2_FLOOR)
-        nc.gpsimd.tensor_tensor(out=e_inv[:], in0=e_inv[:], in1=minus_half[:], op=ALU.pow)
-        nc.gpsimd.tensor_tensor(out=e_inv2[:], in0=e_inv[:], in1=e_inv[:], op=ALU.mult)
-        for h in range(HALVES):
-            cols = slice(h * BANK, (h + 1) * BANK)
-            nc.vector.quantize_mx(
-                out=e1_codes[:, cols].bitcast(FP8X4),
-                scales=e1_scales[:, cols],
-                in_=e1_grouped[:, h * BANK * 4 : (h + 1) * BANK * 4],
-            )
-
         q_norm2, q_inv, q_grouped, q_codes, q_scales = {}, {}, {}, {}, {}
 
         def square_queries(n):
@@ -167,14 +130,50 @@ def tile_frozenhopfield_pa_t_kernel(tc, q, word_embs, beta, out):
             q_scales[j] = ring.tile([P, PQ], U8, name="q_scales", align_bytes=64)
             nc.vector.quantize_mx(out=q_codes[j][:].bitcast(FP8X4), scales=q_scales[j][:], in_=q_grouped[j][:])
 
+        e_norm2_even = keep.tile([P, V_TILES // 2], F32, name="e_norm2_even")
+        e_norm2_odd = keep.tile([P, V_TILES // 2], F32, name="e_norm2_odd")
+        e_inv = keep.tile([P, V_TILES], F32, name="e_inv")
+        e_inv2 = keep.tile([P, V_TILES], F32, name="e_inv2")
+
+        def column(t):
+            c = t // 2 + (t % 2) * (V_TILES // 2)
+            return slice(c, c + 1)
+
+        e1_grouped = keep.tile([P, V * 4], BF16, name="e1_grouped", align_bytes=64)
+        e1_codes = keep.tile([P, V], U32, name="e1_codes", align_bytes=64)
+        e1_scales = keep.tile([P, V], U8, name="e1_scales", align_bytes=64)
+        for c in range(V_TILES // 2):
+            sum_of_squares_on_scalar(e_rows[:, 2 * c * HID : (2 * c + 1) * HID], e_norm2_even[:, c : c + 1])
+            sum_of_squares_on_vector(e_rows[:, (2 * c + 1) * HID : (2 * c + 2) * HID], e_norm2_odd[:, c : c + 1])
         square_queries(0)
         square_queries(1)
+        for c in range(V_TILES // 2):
+            first = c * BANK
+            contraction_to_partitions(
+                nc, psum_t, nc.scalar.copy if c % 2 else nc.vector.tensor_copy,
+                e_rows[:].bitcast(F32)[:, first : first + BANK],
+                e1_grouped[:].bitcast(F32)[:, first : first + BANK],
+                identity[:],
+            )
+        half = V_TILES // 2
+        nc.gpsimd.tensor_scalar_max(out=e_inv[:, :half], in0=e_norm2_even[:], scalar1=NORM2_FLOOR)
+        nc.gpsimd.tensor_scalar_max(out=e_inv[:, half:], in0=e_norm2_odd[:], scalar1=NORM2_FLOOR)
+        nc.gpsimd.tensor_tensor(out=e_inv[:], in0=e_inv[:], in1=minus_half[:], op=ALU.pow)
+        nc.gpsimd.tensor_tensor(out=e_inv2[:], in0=e_inv[:], in1=e_inv[:], op=ALU.mult)
+        for h in range(HALVES):
+            cols = slice(h * BANK, (h + 1) * BANK)
+            nc.vector.quantize_mx(
+                out=e1_codes[:, cols].bitcast(FP8X4),
+                scales=e1_scales[:, cols],
+                in_=e1_grouped[:, h * BANK * 4 : (h + 1) * BANK * 4],
+            )
+
         flip_queries(0)
+        quantise_queries(0)
         query_norms(0)
 
         table_a = keep.tile([P, V], F32, name="table_a")
         table_b = keep.tile([P, V], F32, name="table_b")
-        inv2_psum = psum_b.tile([P, BANK], F32, name="inv2_psum")
         for h in range(HALVES):
             spread = psum_s.tile([P, BANK], F32, name="spread", tag="dots")
             for s in range(BANK // P):
@@ -187,7 +186,7 @@ def tile_frozenhopfield_pa_t_kernel(tc, q, word_embs, beta, out):
                 out=table_a[:, cols], in0=spread[:], scalar1=float(beta), scalar2=None, op0=ALU.mult
             )
         for h in range(HALVES):
-            spread = inv2_psum if h == 0 else psum_s.tile([P, BANK], F32, name="spread", tag="dots")
+            spread = psum_s.tile([P, BANK], F32, name="spread", tag="dots")
             for s in range(BANK // P):
                 nc.tensor.transpose(
                     spread[:, s * P : (s + 1) * P],
@@ -197,7 +196,7 @@ def tile_frozenhopfield_pa_t_kernel(tc, q, word_embs, beta, out):
             nc.scalar.activation(out=table_b[:, cols], in_=spread[:], func=ACT.Copy, scale=-EPS * float(beta))
 
         factor, dots, x, minus_max, prob, p_flip, p_grouped, p_codes, p_scales = {}, {}, {}, {}, {}, {}, {}, {}, {}
-        row_sum, inv_sum, mixed, results, q_minus = {}, {}, {}, {}, {}
+        row_sum, inv_sum, mixed, results = {}, {}, {}, {}
 
         def inverse_query_norm(n):
             j, i = divmod(n, PAIR)
@@ -223,7 +222,7 @@ def tile_frozenhopfield_pa_t_kernel(tc, q, word_embs, beta, out):
         def factor_on_vector(n):
             cols = slice(0, VECTOR_COLS)
             nc.vector.scalar_tensor_tensor(
-                out=factor[n][:, cols], in0=inv2_psum[:, cols], scalar=q_minus[n // PAIR][:, n % PAIR : n % PAIR + 1],
+                out=factor[n][:, cols], in0=table_b[:, cols], scalar=inverse_query_norm(n),
                 in1=table_a[:, cols], op0=ALU.mult, op1=ALU.add,
             )
             if n == 0:
@@ -232,13 +231,6 @@ def tile_frozenhopfield_pa_t_kernel(tc, q, word_embs, beta, out):
                     out=factor[n][:, cols], in0=table_b[:, cols], scalar=inverse_query_norm(n), in1=table_a[:, cols],
                     op0=ALU.mult, op1=ALU.add,
                 )
-
-        def minus_query_norms(j):
-            q_minus[j] = keep.tile([P, PAIR], F32, name="q_minus%d" % j)
-            nc.gpsimd.tensor_scalar(
-                out=q_minus[j][:], in0=q_inv[j][:], scalar1=-EPS * float(beta), scalar2=0.0,
-                op0=ALU.mult, op1=ALU.add,
-            )
 
         def scores(n, h):
             j, i = divmod(n, PAIR)
@@ -351,20 +343,18 @@ def tile_frozenhopfield_pa_t_kernel(tc, q, word_embs, beta, out):
             if tile_exists(n - 4):
                 mix(n - 4)
                 finish(n - 4)
-            if pair_exists(k + 2) and i == 0:
-                if k + 2 > 0:
-                    query_norms(k + 2)
-                minus_query_norms(k + 2)
             if tile_exists(n + 3):
                 factor_on_gpsimd(n + 3)
-            if tile_exists(n + 1):
-                scale(n + 1, 0)
-                scale(n + 1, 1)
+            if 0 < k + 2 < N_PAIRS and i == 0:
+                query_norms(k + 2)
             if tile_exists(n + 2):
                 scores(n + 2, 0)
                 scores(n + 2, 1)
             if tile_exists(n):
                 row_maximum(n)
+            if tile_exists(n + 1):
+                scale(n + 1, 0)
+                scale(n + 1, 1)
             if tile_exists(n - 2):
                 flip_prob(n - 2)
             if tile_exists(n + 6):
@@ -377,11 +367,11 @@ def tile_frozenhopfield_pa_t_kernel(tc, q, word_embs, beta, out):
                 quantise_prob(n - 3)
             if tile_exists(n + 2):
                 factor_on_vector(n + 2)
-            if pair_exists(k + 2) and i == 0:
+            if 0 < k + 2 < N_PAIRS and i == 1:
                 quantise_queries(k + 2)
             if i == 1 and pair_exists(k - 1):
                 invert_sums(k - 1)
-            if n in (-2, 1):
-                group_words(0 if n == -2 else 1)
+            if n in (1, 2):
+                group_words(n - 1)
             if n in (2, 3):
                 quantise_words(n - 2)

@@ -26,7 +26,7 @@ V_TILES = V // P
 BANK = 512
 HALVES = V // BANK
 PASSES = V // 512
-VECTOR_COLS = 512
+VECTOR_COLS = 640
 PIECE = 512
 
 FLOPS = 2 * 2 * B * V * HID
@@ -303,11 +303,19 @@ def tile_frozenhopfield_pa_t_kernel(tc, q, word_embs, beta, out):
             j, i = divmod(n, PAIR)
             if i == 0:
                 results[j] = ring.tile([P, PAIR * HID], F32, name="results")
-            nc.scalar.activation(
-                out=results[j][:, i * HID : (i + 1) * HID], in_=mixed[n][:], func=ACT.Copy,
-                scale=inv_sum[j][:, i : i + 1],
-            )
-            if i == PAIR - 1:
+            cols = slice(i * HID, (i + 1) * HID)
+            if n in (N_TILES - 4, N_TILES - 2):
+                nc.vector.tensor_scalar(
+                    out=results[j][:, cols], in0=mixed[n][:], scalar1=inv_sum[j][:, i : i + 1], scalar2=None,
+                    op0=ALU.mult,
+                )
+            else:
+                nc.scalar.activation(
+                    out=results[j][:, cols], in_=mixed[n][:], func=ACT.Copy, scale=inv_sum[j][:, i : i + 1]
+                )
+            if n >= N_TILES - PAIR:
+                nc.sync.dma_start(out=out_rows[:, n, :], in_=results[j][:, cols])
+            elif i == PAIR - 1:
                 nc.sync.dma_start(
                     out=out_rows[:, j * PAIR : (j + 1) * PAIR, :],
                     in_=results[j][:].rearrange("p (s n) -> p s n", s=PAIR),

@@ -26,8 +26,10 @@ V_TILES = V // P
 BANK = 512
 HALVES = V // BANK
 PASSES = V // 512
-VECTOR_COLS = 640
-PIECE = 512
+TENSOR_COLS = 256
+FIRST_ON_TENSOR = 6
+NORM_BUFS = 3
+QUADRANT = 32
 
 FLOPS = 2 * 2 * B * V * HID
 
@@ -61,8 +63,8 @@ def tile_frozenhopfield_pa_t_kernel(tc, q, word_embs, beta, out):
         tc.tile_pool(name="keep", bufs=1) as keep,
         tc.tile_pool(name="ring", bufs=3) as ring,
         tc.psum_pool(name="psum_s", bufs=4) as psum_s,
-        tc.psum_pool(name="psum_t", bufs=2) as psum_t,
-        tc.psum_pool(name="psum_o", bufs=2) as psum_o,
+        tc.psum_pool(name="psum_t", bufs=3) as psum_t,
+        tc.psum_pool(name="psum_o", bufs=1) as psum_o,
         tc.manual_schedule(),
     ):
         q_loaded = []
@@ -93,6 +95,12 @@ def tile_frozenhopfield_pa_t_kernel(tc, q, word_embs, beta, out):
 
         identity = keep.tile([P, P], F32, name="identity")
         make_identity(nc, identity[:])
+        identity16 = keep.tile([P, P], BF16, name="identity16")
+        make_identity(nc, identity16[:])
+        norm_rows = []
+        for r in range(NORM_BUFS):
+            norm_rows.append(keep.tile([P, PQ], BF16, name="norm_rows%d" % r))
+            nc.gpsimd.memset(norm_rows[r][:], 1.0 / QUADRANT)
         minus_half = keep.tile([P, V_TILES], F32, name="minus_half")
         nc.vector.memset(minus_half[:], -0.5)
 
@@ -106,7 +114,7 @@ def tile_frozenhopfield_pa_t_kernel(tc, q, word_embs, beta, out):
                 out=products[:], in0=rows, scalar=1.0, in1=rows, op0=ALU.mult, op1=ALU.mult, accum_out=norm2
             )
 
-        q_norm2, q_inv, q_grouped, q_codes, q_scales = {}, {}, {}, {}, {}
+        q_norm2, q_inv, q_inv16, q_grouped, q_codes, q_scales = {}, {}, {}, {}, {}, {}
 
         def square_queries(n):
             j, i = divmod(n, PAIR)
@@ -124,27 +132,26 @@ def tile_frozenhopfield_pa_t_kernel(tc, q, word_embs, beta, out):
             q_inv[j] = keep.tile([P, PAIR], F32, name="q_inv%d" % j)
             nc.gpsimd.tensor_scalar_max(out=q_inv[j][:], in0=q_norm2[j][:], scalar1=NORM2_FLOOR)
             nc.gpsimd.tensor_tensor(out=q_inv[j][:], in0=q_inv[j][:], in1=minus_half[:, :PAIR], op=ALU.pow)
+            if j >= FIRST_ON_TENSOR // PAIR:
+                q_inv16[j] = keep.tile([P, PAIR], BF16, name="q_inv16_%d" % j)
+                nc.gpsimd.tensor_copy(out=q_inv16[j][:], in_=q_inv[j][:])
 
         def quantise_queries(j):
             q_codes[j] = ring.tile([P, PQ], U32, name="q_codes", align_bytes=64)
             q_scales[j] = ring.tile([P, PQ], U8, name="q_scales", align_bytes=64)
             nc.vector.quantize_mx(out=q_codes[j][:].bitcast(FP8X4), scales=q_scales[j][:], in_=q_grouped[j][:])
 
-        e_norm2_even = keep.tile([P, V_TILES // 2], F32, name="e_norm2_even")
-        e_norm2_odd = keep.tile([P, V_TILES // 2], F32, name="e_norm2_odd")
+        e_norm2 = keep.tile([P, V_TILES], F32, name="e_norm2")
         e_inv = keep.tile([P, V_TILES], F32, name="e_inv")
-        e_inv2 = keep.tile([P, V_TILES], F32, name="e_inv2")
-
-        def column(t):
-            c = t // 2 + (t % 2) * (V_TILES // 2)
-            return slice(c, c + 1)
 
         e1_grouped = keep.tile([P, V * 4], BF16, name="e1_grouped", align_bytes=64)
         e1_codes = keep.tile([P, V], U32, name="e1_codes", align_bytes=64)
         e1_scales = keep.tile([P, V], U8, name="e1_scales", align_bytes=64)
         for c in range(V_TILES // 2):
-            sum_of_squares_on_scalar(e_rows[:, 2 * c * HID : (2 * c + 1) * HID], e_norm2_even[:, c : c + 1])
-            sum_of_squares_on_vector(e_rows[:, (2 * c + 1) * HID : (2 * c + 2) * HID], e_norm2_odd[:, c : c + 1])
+            sum_of_squares_on_scalar(e_rows[:, 2 * c * HID : (2 * c + 1) * HID], e_norm2[:, 2 * c : 2 * c + 1])
+            sum_of_squares_on_vector(e_rows[:, (2 * c + 1) * HID : (2 * c + 2) * HID], e_norm2[:, 2 * c + 1 : 2 * c + 2])
+        nc.vector.tensor_scalar_max(out=e_norm2[:], in0=e_norm2[:], scalar1=NORM2_FLOOR)
+        nc.gpsimd.tensor_tensor(out=e_inv[:], in0=e_norm2[:], in1=minus_half[:], op=ALU.pow)
         square_queries(0)
         square_queries(1)
         for c in range(V_TILES // 2):
@@ -155,11 +162,6 @@ def tile_frozenhopfield_pa_t_kernel(tc, q, word_embs, beta, out):
                 e1_grouped[:].bitcast(F32)[:, first : first + BANK],
                 identity[:],
             )
-        half = V_TILES // 2
-        nc.gpsimd.tensor_scalar_max(out=e_inv[:, :half], in0=e_norm2_even[:], scalar1=NORM2_FLOOR)
-        nc.gpsimd.tensor_scalar_max(out=e_inv[:, half:], in0=e_norm2_odd[:], scalar1=NORM2_FLOOR)
-        nc.gpsimd.tensor_tensor(out=e_inv[:], in0=e_inv[:], in1=minus_half[:], op=ALU.pow)
-        nc.gpsimd.tensor_tensor(out=e_inv2[:], in0=e_inv[:], in1=e_inv[:], op=ALU.mult)
         for h in range(HALVES):
             cols = slice(h * BANK, (h + 1) * BANK)
             nc.vector.quantize_mx(
@@ -172,65 +174,85 @@ def tile_frozenhopfield_pa_t_kernel(tc, q, word_embs, beta, out):
         quantise_queries(0)
         query_norms(0)
 
-        table_a = keep.tile([P, V], F32, name="table_a")
+        minus_a = keep.tile([P, V], F32, name="minus_a")
         table_b = keep.tile([P, V], F32, name="table_b")
         for h in range(HALVES):
             spread = psum_s.tile([P, BANK], F32, name="spread", tag="dots")
             for s in range(BANK // P):
+                t = h * (BANK // P) + s
                 nc.tensor.transpose(
-                    spread[:, s * P : (s + 1) * P],
-                    e_inv[:, column(h * (BANK // P) + s)].to_broadcast([P, P]), identity[:],
+                    spread[:, s * P : (s + 1) * P], e_inv[:, t : t + 1].to_broadcast([P, P]), identity[:]
                 )
             cols = slice(h * BANK, (h + 1) * BANK)
             nc.vector.tensor_scalar(
-                out=table_a[:, cols], in0=spread[:], scalar1=float(beta), scalar2=None, op0=ALU.mult
+                out=minus_a[:, cols], in0=spread[:], scalar1=-float(beta), scalar2=None, op0=ALU.mult
             )
-        for h in range(HALVES):
-            spread = psum_s.tile([P, BANK], F32, name="spread", tag="dots")
-            for s in range(BANK // P):
-                nc.tensor.transpose(
-                    spread[:, s * P : (s + 1) * P],
-                    e_inv2[:, column(h * (BANK // P) + s)].to_broadcast([P, P]), identity[:],
-                )
-            cols = slice(h * BANK, (h + 1) * BANK)
-            nc.scalar.activation(out=table_b[:, cols], in_=spread[:], func=ACT.Copy, scale=-EPS * float(beta))
+            nc.scalar.activation(
+                out=table_b[:, cols], in_=spread[:], func=ACT.Square, scale=(EPS * float(beta)) ** 0.5
+            )
 
-        factor, dots, x, minus_max, prob, p_flip, p_grouped, p_codes, p_scales = {}, {}, {}, {}, {}, {}, {}, {}, {}
-        row_sum, inv_sum, mixed, results = {}, {}, {}, {}
+        tensor_cols = slice(V - TENSOR_COLS, V)
+        factor_rhs = keep.tile([P, TENSOR_COLS], BF16, name="factor_rhs")
+        part = keep.tile([P, TENSOR_COLS], BF16, name="part")
+        rest = keep.tile([P, TENSOR_COLS], F32, name="rest")
+        rest2 = keep.tile([P, TENSOR_COLS], F32, name="rest2")
+        part2 = keep.tile([P, TENSOR_COLS], BF16, name="part2")
+
+        def quadrant(g):
+            return slice(g * QUADRANT, (g + 1) * QUADRANT)
+
+        def build_factor_rhs():
+            nc.gpsimd.tensor_scalar(
+                out=factor_rhs[quadrant(0), :], in0=table_b[quadrant(0), tensor_cols], scalar1=1.0 / QUADRANT, scalar2=0.0,
+                op0=ALU.mult, op1=ALU.add,
+            )
+            nc.gpsimd.tensor_copy(out=part[:], in_=minus_a[:, tensor_cols])
+            nc.gpsimd.tensor_tensor(out=rest[:], in0=minus_a[:, tensor_cols], in1=part[:], op=ALU.subtract)
+            nc.gpsimd.tensor_copy(out=part2[:], in_=rest[:])
+            nc.gpsimd.tensor_tensor(out=rest2[:], in0=rest[:], in1=part2[:], op=ALU.subtract)
+            nc.gpsimd.tensor_copy(out=factor_rhs[quadrant(1), :], in_=part[quadrant(1), :])
+            nc.gpsimd.tensor_copy(out=factor_rhs[quadrant(2), :], in_=part2[quadrant(2), :])
+            nc.gpsimd.tensor_copy(out=factor_rhs[quadrant(3), :], in_=rest2[quadrant(3), :])
+
+        factor, dots, minus_x, minus_max, prob, p_flip, p_grouped, p_codes, p_scales = {}, {}, {}, {}, {}, {}, {}, {}, {}
+        row_sum, inv_sum, mixed, results, factor_psum = {}, {}, {}, {}, {}
 
         def inverse_query_norm(n):
             j, i = divmod(n, PAIR)
             return q_inv[j][:, i : i + 1]
 
-        def factor_on_gpsimd(n):
-            factor[n] = ring.tile([P, V], F32, name="factor", bufs=4)
-            if n == 0:
-                return
-            pieces = []
-            for first in range(VECTOR_COLS, V, PIECE):
-                pieces.append(slice(first, min(first + PIECE, V)))
-            for cols in pieces:
-                nc.gpsimd.tensor_scalar(
-                    out=factor[n][:, cols], in0=table_b[:, cols], scalar1=inverse_query_norm(n), scalar2=0.0,
-                    op0=ALU.mult, op1=ALU.add,
-                )
-            for cols in pieces:
-                nc.gpsimd.tensor_tensor(
-                    out=factor[n][:, cols], in0=factor[n][:, cols], in1=table_a[:, cols], op=ALU.add
-                )
+        def vector_cols(n):
+            return V - TENSOR_COLS if n >= FIRST_ON_TENSOR else V
 
         def factor_on_vector(n):
-            cols = slice(0, VECTOR_COLS)
+            factor[n] = ring.tile([P, V], F32, name="factor", bufs=4)
+            cols = slice(0, vector_cols(n))
             nc.vector.scalar_tensor_tensor(
-                out=factor[n][:, cols], in0=table_b[:, cols], scalar=inverse_query_norm(n),
-                in1=table_a[:, cols], op0=ALU.mult, op1=ALU.add,
+                out=factor[n][:, cols], in0=table_b[:, cols], scalar=inverse_query_norm(n), in1=minus_a[:, cols],
+                op0=ALU.mult, op1=ALU.add,
             )
-            if n == 0:
-                cols = slice(VECTOR_COLS, V)
-                nc.vector.scalar_tensor_tensor(
-                    out=factor[n][:, cols], in0=table_b[:, cols], scalar=inverse_query_norm(n), in1=table_a[:, cols],
-                    op0=ALU.mult, op1=ALU.add,
+
+        def factor_on_tensor(n):
+            if vector_cols(n) == V:
+                return
+            j, i = divmod(n, PAIR)
+            factor_psum[n] = psum_t.tile([P, BANK], F32, name="factor_psum", tag="flipped")
+            nc.tensor.matmul(
+                factor_psum[n][:, :TENSOR_COLS], norm_rows[j % NORM_BUFS][:, i * P : (i + 1) * P], factor_rhs[:], start=True, stop=True
+            )
+
+        def factor_to_sbuf(n):
+            if vector_cols(n) == V:
+                return
+            nc.scalar.copy(out=factor[n][:, V - TENSOR_COLS :], in_=factor_psum[n][:, :TENSOR_COLS])
+
+        def spread_norms(j):
+            spread = psum_t.tile([P, PQ], BF16, name="spread", tag="flipped")
+            for i in range(PAIR):
+                nc.tensor.transpose(
+                    spread[:, i * P : (i + 1) * P], q_inv16[j][:, i : i + 1].to_broadcast([P, P]), identity16[:]
                 )
+            nc.scalar.copy(out=norm_rows[j % NORM_BUFS][:QUADRANT, :], in_=spread[:QUADRANT, :])
 
         def scores(n, h):
             j, i = divmod(n, PAIR)
@@ -249,16 +271,16 @@ def tile_frozenhopfield_pa_t_kernel(tc, q, word_embs, beta, out):
 
         def scale(n, h):
             if h == 0:
-                x[n] = ring.tile([P, V], F32, name="x")
+                minus_x[n] = ring.tile([P, V], F32, name="minus_x")
             cols = slice(h * BANK, (h + 1) * BANK)
             nc.vector.scalar_tensor_tensor(
-                out=x[n][:, cols], in0=dots[n, h][:], scalar=inverse_query_norm(n), in1=factor[n][:, cols],
+                out=minus_x[n][:, cols], in0=dots[n, h][:], scalar=inverse_query_norm(n), in1=factor[n][:, cols],
                 op0=ALU.mult, op1=ALU.mult,
             )
 
         def row_maximum(n):
             minus_max[n] = ring.tile([P, 1], F32, name="minus_max")
-            nc.vector.tensor_reduce(out=minus_max[n][:], in_=x[n][:], axis=AXIS.X, op=ALU.max, negate=True)
+            nc.vector.tensor_reduce(out=minus_max[n][:], in_=minus_x[n][:], axis=AXIS.X, op=ALU.min)
 
         def soften(n):
             j, i = divmod(n, PAIR)
@@ -266,7 +288,7 @@ def tile_frozenhopfield_pa_t_kernel(tc, q, word_embs, beta, out):
                 row_sum[j] = ring.tile([P, PAIR], F32, name="row_sum")
             prob[n] = ring.tile([P, V], BF16, name="prob")
             nc.scalar.activation(
-                out=prob[n][:], in_=x[n][:], func=ACT.Exp, bias=minus_max[n][:], scale=1.0,
+                out=prob[n][:], in_=minus_x[n][:], func=ACT.Exp, bias=minus_max[n][:], scale=-1.0,
                 accum_out=row_sum[j][:, i : i + 1],
             )
 
@@ -325,10 +347,12 @@ def tile_frozenhopfield_pa_t_kernel(tc, q, word_embs, beta, out):
         e2_codes = keep.tile([P, PASSES * HID], U32, name="e2_codes", align_bytes=64)
         e2_scales = keep.tile([P, PASSES * HID], U8, name="e2_scales", align_bytes=64)
 
-        def group_words(g):
+        def group_words(piece):
+            g, half = divmod(piece, 2)
+            rows = slice(half * (HID // 2), (half + 1) * (HID // 2))
             nc.scalar.copy(
-                out=e2_grouped[:, g * HID * 4 : (g + 1) * HID * 4].rearrange("p (n t) -> p n t", t=4),
-                in_=e_by_word[:, g * HID * 4 : (g + 1) * HID * 4].rearrange("p (t n) -> p n t", t=4),
+                out=e2_grouped[:, g * HID * 4 : (g + 1) * HID * 4].rearrange("p (n t) -> p n t", t=4)[:, rows, :],
+                in_=e_by_word[:, g * HID * 4 : (g + 1) * HID * 4].rearrange("p (t n) -> p n t", t=4)[:, rows, :],
             )
 
         def quantise_words(g):
@@ -351,15 +375,12 @@ def tile_frozenhopfield_pa_t_kernel(tc, q, word_embs, beta, out):
             if tile_exists(n - 4):
                 mix(n - 4)
                 finish(n - 4)
-            if tile_exists(n + 3):
-                factor_on_gpsimd(n + 3)
             if 0 < k + 2 < N_PAIRS and i == 0:
                 query_norms(k + 2)
-            if tile_exists(n + 2):
-                scores(n + 2, 0)
-                scores(n + 2, 1)
             if tile_exists(n):
                 row_maximum(n)
+            if tile_exists(n - 3):
+                quantise_prob(n - 3)
             if tile_exists(n + 1):
                 scale(n + 1, 0)
                 scale(n + 1, 1)
@@ -371,15 +392,24 @@ def tile_frozenhopfield_pa_t_kernel(tc, q, word_embs, beta, out):
                 group_prob(n - 2)
             if pair_exists(k + 3) and i == 1:
                 flip_queries(k + 3)
-            if tile_exists(n - 3):
-                quantise_prob(n - 3)
+            if tile_exists(n + 2):
+                scores(n + 2, 0)
+                scores(n + 2, 1)
+            if pair_exists(k + 2) and i == 1 and k + 2 >= FIRST_ON_TENSOR // PAIR:
+                spread_norms(k + 2)
+            if tile_exists(n + 2):
+                factor_on_tensor(n + 2)
             if tile_exists(n + 2):
                 factor_on_vector(n + 2)
+                factor_to_sbuf(n + 2)
             if 0 < k + 2 < N_PAIRS and i == 1:
                 quantise_queries(k + 2)
             if i == 1 and pair_exists(k - 1):
                 invert_sums(k - 1)
-            if n in (1, 2):
-                group_words(n - 1)
+            if n == 2:
+                build_factor_rhs()
+            if n in (0, 1, 2, 3):
+                for piece in (n,):
+                    group_words(piece)
             if n in (2, 3):
                 quantise_words(n - 2)

import concourse.mybir as mybir
from concourse.masks import make_identity

F32 = mybir.dt.float32
BF16 = mybir.dt.bfloat16
U32 = mybir.dt.uint32
U8 = mybir.dt.uint8
FP8X4 = mybir.dt.float8_e4m3fn_x4
ALU = mybir.AluOpType
ACT = mybir.ActivationFunctionType
AXIS = mybir.AxisListType

P = 128
B = 4096
V = 1024
HID = 512
EPS = 1e-8
NORM2_FLOOR = 1e-24

WORDS = 256
N_TILES = B // P
PAIR = 2
N_PAIRS = N_TILES // PAIR
PQ = PAIR * P
V_TILES = V // P
BANK = 512
HALVES = V // BANK
PASSES = V // 512
TENSOR_COLS = 256
FIRST_ON_TENSOR = 6
NORM_BUFS = 3
QUADRANT = 32

FLOPS = 2 * 2 * B * V * HID


def contraction_to_partitions(nc, psum, copy, rows_words, grouped_words, identity):
    flip_rows(nc, psum, rows_words, identity)(copy, grouped_words)


def flip_rows(nc, psum, rows_words, identity):
    chunks = rows_words.shape[1] // WORDS
    flipped = psum.tile([P, chunks * WORDS], F32, name="flipped")
    for piece in range(2 * chunks):
        cols = slice(piece * P, (piece + 1) * P)
        nc.tensor.transpose(flipped[:, cols], rows_words[:, cols], identity)

    def copy_out(copy, grouped_words):
        copy(
            out=grouped_words.rearrange("p (c r u) -> p c r u", c=chunks, u=2),
            in_=flipped[:].rearrange("p (c u r) -> p c r u", c=chunks, u=2),
        )

    return copy_out


def tile_frozenhopfield_pa_t_kernel(tc, q, word_embs, beta, out):
    nc = tc.nc
    q_rows = q.rearrange("(p i) k -> p i k", i=N_TILES)
    out_rows = out.rearrange("(p i) n -> p i n", i=N_TILES)

    with (
        tc.tile_pool(name="keep", bufs=1) as keep,
        tc.tile_pool(name="ring", bufs=3) as ring,
        tc.psum_pool(name="psum_s", bufs=4) as psum_s,
        tc.psum_pool(name="psum_t", bufs=3) as psum_t,
        tc.psum_pool(name="psum_o", bufs=1) as psum_o,
        tc.manual_schedule(),
    ):
        q_loaded = []
        for j in range(N_PAIRS):
            q_loaded.append(keep.tile([P, PAIR * HID], BF16, name="q_loaded%d" % j))

        def load_queries(j):
            nc.sync.dma_start(
                out=q_loaded[j][:].rearrange("p (i k) -> p i k", i=PAIR),
                in_=q_rows[:, j * PAIR : (j + 1) * PAIR, :],
            )

        e_rows = keep.tile([P, V_TILES * HID], BF16, name="e_rows")
        e_src = word_embs.rearrange("(t p) k -> p t k", p=P)
        e_dst = e_rows[:].rearrange("p (t k) -> p t k", t=V_TILES)
        for quarter in range(4):
            tiles = slice(2 * quarter, 2 * quarter + 2)
            nc.sync.dma_start(out=e_dst[:, tiles, :], in_=e_src[:, tiles, :])
        load_queries(0)
        load_queries(1)
        e_by_word = keep.tile([P, V_TILES * HID], BF16, name="e_by_word")
        nc.sync.dma_start(
            out=e_by_word[:].rearrange("p (c e n) -> p c e n", c=4, e=2),
            in_=word_embs.rearrange("(c p e) n -> p c e n", c=4, e=2),
        )
        for j in range(2, N_PAIRS):
            load_queries(j)

        identity = keep.tile([P, P], F32, name="identity")
        make_identity(nc, identity[:])
        identity16 = keep.tile([P, P], BF16, name="identity16")
        make_identity(nc, identity16[:])
        norm_rows = []
        for r in range(NORM_BUFS):
            norm_rows.append(keep.tile([P, PQ], BF16, name="norm_rows%d" % r))
            nc.gpsimd.memset(norm_rows[r][:], 1.0 / QUADRANT)
        minus_half = keep.tile([P, V_TILES], F32, name="minus_half")
        nc.vector.memset(minus_half[:], -0.5)

        def sum_of_squares_on_scalar(rows, norm2):
            squares = ring.tile([P, HID], BF16, name="squares")
            nc.scalar.activation(out=squares[:], in_=rows, func=ACT.Square, accum_out=norm2)

        def sum_of_squares_on_vector(rows, norm2):
            products = ring.tile([P, HID], F32, name="products")
            nc.vector.scalar_tensor_tensor(
                out=products[:], in0=rows, scalar=1.0, in1=rows, op0=ALU.mult, op1=ALU.mult, accum_out=norm2
            )

        q_norm2, q_inv, q_inv16, q_grouped, q_codes, q_scales = {}, {}, {}, {}, {}, {}

        def square_queries(n):
            j, i = divmod(n, PAIR)
            if i == 0:
                q_norm2[j] = keep.tile([P, PAIR], F32, name="q_norm2_%d" % j)
            sum_of_squares_on_scalar(q_loaded[j][:, i * HID : (i + 1) * HID], q_norm2[j][:, i : i + 1])

        def flip_queries(j):
            q_grouped[j] = ring.tile([P, PAIR * HID], BF16, name="q_grouped", align_bytes=64)
            contraction_to_partitions(
                nc, psum_t, nc.scalar.copy, q_loaded[j][:].bitcast(F32), q_grouped[j][:].bitcast(F32), identity[:]
            )

        def query_norms(j):
            q_inv[j] = keep.tile([P, PAIR], F32, name="q_inv%d" % j)
            nc.gpsimd.tensor_scalar_max(out=q_inv[j][:], in0=q_norm2[j][:], scalar1=NORM2_FLOOR)
            nc.gpsimd.tensor_tensor(out=q_inv[j][:], in0=q_inv[j][:], in1=minus_half[:, :PAIR], op=ALU.pow)
            if j >= FIRST_ON_TENSOR // PAIR:
                q_inv16[j] = keep.tile([P, PAIR], BF16, name="q_inv16_%d" % j)
                nc.gpsimd.tensor_copy(out=q_inv16[j][:], in_=q_inv[j][:])

        def quantise_queries(j):
            q_codes[j] = ring.tile([P, PQ], U32, name="q_codes", align_bytes=64)
            q_scales[j] = ring.tile([P, PQ], U8, name="q_scales", align_bytes=64)
            nc.vector.quantize_mx(out=q_codes[j][:].bitcast(FP8X4), scales=q_scales[j][:], in_=q_grouped[j][:])

        e_norm2 = keep.tile([P, V_TILES], F32, name="e_norm2")
        e_inv = keep.tile([P, V_TILES], F32, name="e_inv")

        e1_grouped = keep.tile([P, V * 4], BF16, name="e1_grouped", align_bytes=64)
        e1_codes = keep.tile([P, V], U32, name="e1_codes", align_bytes=64)
        e1_scales = keep.tile([P, V], U8, name="e1_scales", align_bytes=64)
        for c in range(V_TILES // 2):
            sum_of_squares_on_scalar(e_rows[:, 2 * c * HID : (2 * c + 1) * HID], e_norm2[:, 2 * c : 2 * c + 1])
            sum_of_squares_on_vector(e_rows[:, (2 * c + 1) * HID : (2 * c + 2) * HID], e_norm2[:, 2 * c + 1 : 2 * c + 2])
        nc.vector.tensor_scalar_max(out=e_norm2[:], in0=e_norm2[:], scalar1=NORM2_FLOOR)
        nc.gpsimd.tensor_tensor(out=e_inv[:], in0=e_norm2[:], in1=minus_half[:], op=ALU.pow)
        square_queries(0)
        square_queries(1)
        for c in range(V_TILES // 2):
            first = c * BANK
            contraction_to_partitions(
                nc, psum_t, nc.scalar.copy if c % 2 else nc.vector.tensor_copy,
                e_rows[:].bitcast(F32)[:, first : first + BANK],
                e1_grouped[:].bitcast(F32)[:, first : first + BANK],
                identity[:],
            )
        for h in range(HALVES):
            cols = slice(h * BANK, (h + 1) * BANK)
            nc.vector.quantize_mx(
                out=e1_codes[:, cols].bitcast(FP8X4),
                scales=e1_scales[:, cols],
                in_=e1_grouped[:, h * BANK * 4 : (h + 1) * BANK * 4],
            )

        flip_queries(0)
        quantise_queries(0)
        query_norms(0)

        minus_a = keep.tile([P, V], F32, name="minus_a")
        table_b = keep.tile([P, V], F32, name="table_b")
        for h in range(HALVES):
            spread = psum_s.tile([P, BANK], F32, name="spread", tag="dots")
            for s in range(BANK // P):
                t = h * (BANK // P) + s
                nc.tensor.transpose(
                    spread[:, s * P : (s + 1) * P], e_inv[:, t : t + 1].to_broadcast([P, P]), identity[:]
                )
            cols = slice(h * BANK, (h + 1) * BANK)
            nc.vector.tensor_scalar(
                out=minus_a[:, cols], in0=spread[:], scalar1=-float(beta), scalar2=None, op0=ALU.mult
            )
            nc.scalar.activation(
                out=table_b[:, cols], in_=spread[:], func=ACT.Square, scale=(EPS * float(beta)) ** 0.5
            )

        tensor_cols = slice(V - TENSOR_COLS, V)
        factor_rhs = keep.tile([P, TENSOR_COLS], BF16, name="factor_rhs")
        part = keep.tile([P, TENSOR_COLS], BF16, name="part")
        rest = keep.tile([P, TENSOR_COLS], F32, name="rest")
        rest2 = keep.tile([P, TENSOR_COLS], F32, name="rest2")
        part2 = keep.tile([P, TENSOR_COLS], BF16, name="part2")

        def quadrant(g):
            return slice(g * QUADRANT, (g + 1) * QUADRANT)

        def build_factor_rhs():
            nc.gpsimd.tensor_scalar(
                out=factor_rhs[quadrant(0), :], in0=table_b[quadrant(0), tensor_cols], scalar1=1.0 / QUADRANT, scalar2=0.0,
                op0=ALU.mult, op1=ALU.add,
            )
            nc.gpsimd.tensor_copy(out=part[:], in_=minus_a[:, tensor_cols])
            nc.gpsimd.tensor_tensor(out=rest[:], in0=minus_a[:, tensor_cols], in1=part[:], op=ALU.subtract)
            nc.gpsimd.tensor_copy(out=part2[:], in_=rest[:])
            nc.gpsimd.tensor_tensor(out=rest2[:], in0=rest[:], in1=part2[:], op=ALU.subtract)
            nc.gpsimd.tensor_copy(out=factor_rhs[quadrant(1), :], in_=part[quadrant(1), :])
            nc.gpsimd.tensor_copy(out=factor_rhs[quadrant(2), :], in_=part2[quadrant(2), :])
            nc.gpsimd.tensor_copy(out=factor_rhs[quadrant(3), :], in_=rest2[quadrant(3), :])

        factor, dots, minus_x, minus_max, prob, p_flip, p_grouped, p_codes, p_scales = {}, {}, {}, {}, {}, {}, {}, {}, {}
        row_sum, inv_sum, mixed, results, factor_psum = {}, {}, {}, {}, {}

        def inverse_query_norm(n):
            j, i = divmod(n, PAIR)
            return q_inv[j][:, i : i + 1]

        def vector_cols(n):
            return V - TENSOR_COLS if n >= FIRST_ON_TENSOR else V

        def factor_on_vector(n):
            factor[n] = ring.tile([P, V], F32, name="factor", bufs=4)
            cols = slice(0, vector_cols(n))
            nc.vector.scalar_tensor_tensor(
                out=factor[n][:, cols], in0=table_b[:, cols], scalar=inverse_query_norm(n), in1=minus_a[:, cols],
                op0=ALU.mult, op1=ALU.add,
            )

        def factor_on_tensor(n):
            if vector_cols(n) == V:
                return
            j, i = divmod(n, PAIR)
            factor_psum[n] = psum_t.tile([P, BANK], F32, name="factor_psum", tag="flipped")
            nc.tensor.matmul(
                factor_psum[n][:, :TENSOR_COLS], norm_rows[j % NORM_BUFS][:, i * P : (i + 1) * P], factor_rhs[:], start=True, stop=True
            )

        def factor_to_sbuf(n):
            if vector_cols(n) == V:
                return
            nc.scalar.copy(out=factor[n][:, V - TENSOR_COLS :], in_=factor_psum[n][:, :TENSOR_COLS])

        def spread_norms(j):
            spread = psum_t.tile([P, PQ], BF16, name="spread", tag="flipped")
            for i in range(PAIR):
                nc.tensor.transpose(
                    spread[:, i * P : (i + 1) * P], q_inv16[j][:, i : i + 1].to_broadcast([P, P]), identity16[:]
                )
            nc.scalar.copy(out=norm_rows[j % NORM_BUFS][:QUADRANT, :], in_=spread[:QUADRANT, :])

        def scores(n, h):
            j, i = divmod(n, PAIR)
            rows = slice(i * P, (i + 1) * P)
            cols = slice(h * BANK, (h + 1) * BANK)
            dots[n, h] = psum_s.tile([P, BANK], F32, name="dots")
            nc.tensor.matmul_mx(
                out=dots[n, h][:],
                lhsT=q_codes[j][:, rows].bitcast(FP8X4),
                lhsT_scale=q_scales[j][:, rows],
                rhs=e1_codes[:, cols].bitcast(FP8X4),
                rhs_scale=e1_scales[:, cols],
                start=True,
                stop=True,
            )

        def scale(n, h):
            if h == 0:
                minus_x[n] = ring.tile([P, V], F32, name="minus_x")
            cols = slice(h * BANK, (h + 1) * BANK)
            nc.vector.scalar_tensor_tensor(
                out=minus_x[n][:, cols], in0=dots[n, h][:], scalar=inverse_query_norm(n), in1=factor[n][:, cols],
                op0=ALU.mult, op1=ALU.mult,
            )

        def row_maximum(n):
            minus_max[n] = ring.tile([P, 1], F32, name="minus_max")
            nc.vector.tensor_reduce(out=minus_max[n][:], in_=minus_x[n][:], axis=AXIS.X, op=ALU.min)

        def soften(n):
            j, i = divmod(n, PAIR)
            if i == 0:
                row_sum[j] = ring.tile([P, PAIR], F32, name="row_sum")
            prob[n] = ring.tile([P, V], BF16, name="prob")
            nc.scalar.activation(
                out=prob[n][:], in_=minus_x[n][:], func=ACT.Exp, bias=minus_max[n][:], scale=-1.0,
                accum_out=row_sum[j][:, i : i + 1],
            )

        def flip_prob(n):
            p_flip[n] = flip_rows(nc, psum_t, prob[n][:].bitcast(F32), identity[:])

        def group_prob(n):
            p_grouped[n] = ring.tile([P, V], BF16, name="p_grouped", align_bytes=64)
            p_flip[n](nc.scalar.copy, p_grouped[n][:].bitcast(F32))

        def quantise_prob(n):
            p_codes[n] = ring.tile([P, PASSES * P], U32, name="p_codes", align_bytes=64)
            p_scales[n] = ring.tile([P, PASSES * P], U8, name="p_scales", align_bytes=64)
            nc.vector.quantize_mx(out=p_codes[n][:].bitcast(FP8X4), scales=p_scales[n][:], in_=p_grouped[n][:])

        def invert_sums(j):
            inv_sum[j] = ring.tile([P, PAIR], F32, name="inv_sum")
            nc.vector.reciprocal(out=inv_sum[j][:], in_=row_sum[j][:])

        def mix(n):
            mixed[n] = psum_o.tile([P, HID], F32, name="mixed")
            for g in range(PASSES):
                nc.tensor.matmul_mx(
                    out=mixed[n][:],
                    lhsT=p_codes[n][:, g * P : (g + 1) * P].bitcast(FP8X4),
                    lhsT_scale=p_scales[n][:, g * P : (g + 1) * P],
                    rhs=e2_codes[:, g * HID : (g + 1) * HID].bitcast(FP8X4),
                    rhs_scale=e2_scales[:, g * HID : (g + 1) * HID],
                    start=(g == 0),
                    stop=(g == PASSES - 1),
                )

        def finish(n):
            j, i = divmod(n, PAIR)
            if i == 0:
                results[j] = ring.tile([P, PAIR * HID], F32, name="results")
            cols = slice(i * HID, (i + 1) * HID)
            if n in (N_TILES - 4, N_TILES - 2):
                nc.vector.tensor_scalar(
                    out=results[j][:, cols], in0=mixed[n][:], scalar1=inv_sum[j][:, i : i + 1], scalar2=None,
                    op0=ALU.mult,
                )
            else:
                nc.scalar.activation(
                    out=results[j][:, cols], in_=mixed[n][:], func=ACT.Copy, scale=inv_sum[j][:, i : i + 1]
                )
            if n >= N_TILES - PAIR:
                nc.sync.dma_start(out=out_rows[:, n, :], in_=results[j][:, cols])
            elif i == PAIR - 1:
                nc.sync.dma_start(
                    out=out_rows[:, j * PAIR : (j + 1) * PAIR, :],
                    in_=results[j][:].rearrange("p (s n) -> p s n", s=PAIR),
                )

        e2_grouped = keep.tile([P, PASSES * HID * 4], BF16, name="e2_grouped", align_bytes=64)
        e2_codes = keep.tile([P, PASSES * HID], U32, name="e2_codes", align_bytes=64)
        e2_scales = keep.tile([P, PASSES * HID], U8, name="e2_scales", align_bytes=64)

        def group_words(piece):
            g, half = divmod(piece, 2)
            rows = slice(half * (HID // 2), (half + 1) * (HID // 2))
            nc.scalar.copy(
                out=e2_grouped[:, g * HID * 4 : (g + 1) * HID * 4].rearrange("p (n t) -> p n t", t=4)[:, rows, :],
                in_=e_by_word[:, g * HID * 4 : (g + 1) * HID * 4].rearrange("p (t n) -> p n t", t=4)[:, rows, :],
            )

        def quantise_words(g):
            nc.vector.quantize_mx(
                out=e2_codes[:, g * HID : (g + 1) * HID].bitcast(FP8X4),
                scales=e2_scales[:, g * HID : (g + 1) * HID],
                in_=e2_grouped[:, g * HID * 4 : (g + 1) * HID * 4],
            )

        def tile_exists(n):
            return 0 <= n < N_TILES

        def pair_exists(j):
            return 0 <= j < N_PAIRS

        for n in range(-4, N_TILES + 5):
            k, i = divmod(n, PAIR)
            if tile_exists(n - 1):
                soften(n - 1)
            if tile_exists(n - 4):
                mix(n - 4)
                finish(n - 4)
            if 0 < k + 2 < N_PAIRS and i == 0:
                query_norms(k + 2)
            if tile_exists(n):
                row_maximum(n)
            if tile_exists(n - 3):
                quantise_prob(n - 3)
            if tile_exists(n + 1):
                scale(n + 1, 0)
                scale(n + 1, 1)
            if tile_exists(n - 2):
                flip_prob(n - 2)
            if tile_exists(n + 6):
                square_queries(n + 6)
            if tile_exists(n - 2):
                group_prob(n - 2)
            if pair_exists(k + 3) and i == 1:
                flip_queries(k + 3)
            if tile_exists(n + 2):
                scores(n + 2, 0)
                scores(n + 2, 1)
            if pair_exists(k + 2) and i == 1 and k + 2 >= FIRST_ON_TENSOR // PAIR:
                spread_norms(k + 2)
            if tile_exists(n + 2):
                factor_on_tensor(n + 2)
            if tile_exists(n + 2):
                factor_on_vector(n + 2)
                factor_to_sbuf(n + 2)
            if 0 < k + 2 < N_PAIRS and i == 1:
                quantise_queries(k + 2)
            if i == 1 and pair_exists(k - 1):
                invert_sums(k - 1)
            if n == 2:
                build_factor_rhs()
            if n in (0, 1, 2, 3):
                for piece in (n,):
                    group_words(piece)
            if n in (2, 3):
                quantise_words(n - 2)
